import numpy as np
import ml_dtypes


def mxq(x, axis, fmt="e4m3"):
    dtype, down = {"e4m3": (ml_dtypes.float8_e4m3fn, 7), "e5m2": (ml_dtypes.float8_e5m2, 14)}[fmt]
    v = np.moveaxis(np.asarray(x, np.float32).astype(ml_dtypes.bfloat16).astype(np.float64), axis, -1)
    blocks = v.reshape(v.shape[:-1] + (-1, 32))
    amax = np.abs(blocks).max(-1, keepdims=True)
    byte = np.maximum(np.where(amax > 0, np.frexp(amax)[1] - 1 + 127, 0) - down, 1)
    scale = np.exp2(byte - 127.0)
    codes = (blocks / scale).astype(np.float32).astype(dtype).astype(np.float64)
    return np.moveaxis((codes * scale).reshape(v.shape), -1, axis)


WIDE = False


def mx_kscale(k):
    if not WIDE:
        return np.ones(k)
    levels = np.array([10, -10, 5, -5, 0])
    a = np.random.permutation(np.resize(levels, k // 512 * 4)).reshape(k // 512, 4)
    idx = np.arange(k)
    return np.exp2(a[idx // 512, idx % 128 // 32])


BF16 = ml_dtypes.bfloat16


def bf(x):
    return np.asarray(x, np.float32).astype(BF16)


def f64(x):
    return np.asarray(x).astype(np.float64)


E2M1 = np.array([0.0, 0.5, 1.0, 1.5, 2.0, 3.0, 4.0, 6.0, -0.0, -0.5, -1.0, -1.5, -2.0, -3.0, -4.0, -6.0])


def pack_weight(w, fmt):
    k, n = w.shape
    w = f64(bf(w)).reshape(k // 32, 32, n)
    amax = np.abs(w).max(1)
    if fmt == "e4m3":
        byte = np.frexp(amax)[1] - 1 + 127 - 7
    else:
        mant, ex = np.frexp(amax / 6.0)
        byte = np.where(mant > 0.5, ex, ex - 1) + 127
    byte = np.clip(np.where(amax > 0, byte, 1), 1, 254)
    scaled = (w * np.exp2(127.0 - byte)[:, None, :]).reshape(k, n).astype(np.float32)
    by_word = np.ascontiguousarray(scaled.reshape(k // 512, 128, 4, n).transpose(0, 1, 3, 2))
    if fmt == "e4m3":
        words = by_word.astype(ml_dtypes.float8_e4m3fn).view(np.uint8)
    else:
        c = by_word.astype(ml_dtypes.float4_e2m1fn).view(np.uint8) & 0xF
        words = c[..., 0::2] | (c[..., 1::2] << 4)
    return np.ascontiguousarray(words), np.ascontiguousarray(byte.astype(np.uint8).reshape(k // 512, 16, n))


def unpack_weight(words, scales, fmt):
    g, p, n, _ = words.shape
    if fmt == "e4m3":
        vals = np.ascontiguousarray(words).view(ml_dtypes.float8_e4m3fn).astype(np.float64)
    else:
        nib = np.empty((g, p, n, 4), np.uint8)
        nib[..., 0::2] = words & 0xF
        nib[..., 1::2] = words >> 4
        vals = E2M1[nib]
    vals = vals * np.repeat(np.exp2(scales.astype(np.float64) - 127.0), 8, axis=1)[..., None]
    return vals.transpose(0, 1, 3, 2).reshape(g * 512, n)


B, S, D, DK, H = 1, 512, 1024, 8192, 8
DH = D // H
LN_EPS = 1e-8


def split_heads(x):
    return x.reshape(B, S, H, DH).transpose(0, 2, 1, 3).reshape(B * H, S, DH)


def merge_heads(x):
    return x.reshape(B, H, S, DH).transpose(0, 2, 1, 3).reshape(B, S, D)


def setup_inputs():
    s = mx_kscale(DK)
    keep = np.random.random((B, S, 1)) > 0.25
    q_relu = bf(np.maximum(np.random.standard_normal((B, S, D)) * 2.2, 0.0))
    k_relu = bf(np.maximum(np.random.standard_normal((B, S, D)) * 2.2, 0.0))
    keys = bf(np.random.standard_normal((B, S, DK)) * s)
    wv = np.random.standard_normal((D, DK)) * 2.2 / np.sqrt(DK) / s[None, :]
    Wv_words, Wv_scales = pack_weight(np.ascontiguousarray(wv.T), "e4m3")
    return {"q_relu": q_relu,
            "k_relu": k_relu,
            "keys": keys,
            "Wv_words": Wv_words,
            "Wv_scales": Wv_scales,
            "bv": bf(np.random.standard_normal(D) * 0.3),
            "queries": bf(np.random.standard_normal((B, S, D)) * keep),
            "ln_gamma": bf(1.0 + 0.1 * np.random.standard_normal(D)),
            "ln_beta": bf(0.1 * np.random.standard_normal(D))}


def reference(q_relu, k_relu, keys, Wv_words, Wv_scales, bv, queries, ln_gamma, ln_beta):
    x = f64(queries)
    v = np.maximum((mxq(f64(keys), 2, "e4m3") @ unpack_weight(Wv_words, Wv_scales, "e4m3")) + f64(bv), 0.0)
    q_, k_, v_ = split_heads(f64(q_relu)), split_heads(f64(k_relu)), split_heads(v)
    sc = q_ @ k_.transpose(0, 2, 1) / np.sqrt(DH)
    e = np.exp(sc - sc.max(-1, keepdims=True))
    mask = np.tile(np.where(np.abs(x).sum(-1, keepdims=True) > 0, 1.0, 0.0), (H, 1, 1))
    o = (mxq(e, 2, "e4m3") @ mxq(v_, 1, "e4m3")) / e.sum(-1, keepdims=True) * mask
    y = merge_heads(o) + x
    mu = y.mean(-1, keepdims=True)
    var = np.square(y - mu).mean(-1, keepdims=True)
    return (y - mu) / np.sqrt(var + LN_EPS) * f64(ln_gamma) + f64(ln_beta)

@@ -1,0 +1,425 @@
+from contextlib import ExitStack
+import math
+
+import concourse.masks as masks
+import concourse.mybir as mybir
+
+F32 = mybir.dt.float32
+BF16 = mybir.dt.bfloat16
+I32 = mybir.dt.int32
+U32 = mybir.dt.uint32
+U8 = mybir.dt.uint8
+FP8X4 = mybir.dt.float8_e4m3fn_x4
+ACT = mybir.ActivationFunctionType
+ALU = mybir.AluOpType
+AXIS = mybir.AxisListType
+
+P = 128
+PACK = 4
+K_PASS = P * PACK
+S = 512
+D = 1024
+DK = 8192
+H = 8
+DH = D // H
+T = S // P
+G = DK // K_PASS
+LN_EPS = 1e-8
+SCORE_SCALE = 1.0 / math.sqrt(DH)
+
+FLOPS = 2 * S * DK * D + 2 * (2 * H * S * S * DH)
+
+PLANES_PER_TILE = 4
+PASSES_PER_LOAD = 2
+LOADS = G // PASSES_PER_LOAD
+RAW_BUFS = 3
+FIRST_HEADS = 3
+UNITS = 2
+PASS_LAG = 2
+STAT_HEADS = 2
+STAT_CHUNKS = H // STAT_HEADS
+BN_STATS_DIM = 6
+BN_AGGR_DIM = 2
+
+
+def tile_multiheadattentionlayer_pa_k_kernel(
+    tc, q_relu, k_relu, keys, Wv_words, Wv_scales, bv, queries, ln_gamma, ln_beta, out
+):
+    nc = tc.nc
+
+    q_rows = q_relu.flatten_outer_dims().rearrange("(p t) d -> p t d", t=T)
+    k_rows = k_relu.flatten_outer_dims().rearrange("(p t) d -> p t d", t=T)
+    x_rows = queries.flatten_outer_dims().rearrange("(p t) d -> p t d", t=T)
+    keys_rows = keys.flatten_outer_dims().rearrange("(p t) k -> p t k", t=T)
+    out_rows = out.flatten_outer_dims().rearrange("(p t) d -> p t d", t=T)
+
+    with ExitStack() as ctx:
+        ctx.enter_context(tc.manual_schedule())
+        keep = ctx.enter_context(tc.tile_pool(name="keep", bufs=1))
+        raw = ctx.enter_context(tc.tile_pool(name="raw", bufs=RAW_BUFS))
+        stage = ctx.enter_context(tc.tile_pool(name="stage", bufs=2))
+        small = ctx.enter_context(tc.tile_pool(name="small", bufs=4))
+        acc_banks = ctx.enter_context(tc.psum_pool(name="acc_banks", bufs=FIRST_HEADS))
+        score_banks = ctx.enter_context(tc.psum_pool(name="score_banks", bufs=2))
+        flip_banks = ctx.enter_context(tc.psum_pool(name="flip_banks", bufs=3))
+
+        w_words = keep.tile([P, G, D], U32, name="w_words", align_bytes=64)
+        w_planes = keep.tile([P, G // PLANES_PER_TILE, D], U8, name="w_planes", align_bytes=64)
+        keys_codes = keep.tile([P, G, S], U32, name="keys_codes", align_bytes=64)
+        keys_scales = keep.tile([P, G, S], U8, name="keys_scales", align_bytes=64)
+        e_codes = keep.tile([P, H, T, P], U32, name="e_codes", align_bytes=64)
+        e_scales = keep.tile([P, H, T, P], U8, name="e_scales", align_bytes=64)
+        v_codes = keep.tile([P, H, DH], U32, name="v_codes", align_bytes=64)
+        v_scales = keep.tile([P, H, DH], U8, name="v_scales", align_bytes=64)
+        q_flipped = keep.tile([P, H, T, P], BF16, name="q_flipped")
+        k_flipped = keep.tile([P, H, S], BF16, name="k_flipped")
+        x_sb = keep.tile([P, T, D], BF16, name="x_sb")
+        y = keep.tile([P, T, D], F32, name="y")
+        gamma_all = keep.tile([P, D], BF16, name="gamma_all")
+        beta_all = keep.tile([P, D], BF16, name="beta_all")
+        ident_bf = keep.tile([P, P], BF16, name="ident_bf")
+        ident_f32 = keep.tile([P, P], F32, name="ident_f32")
+        bv_rows = keep.tile([P, P], BF16, name="bv_rows")
+        bv_cols = keep.tile([P, H], F32, name="bv_cols")
+        table_warm = keep.tile([P, 2], F32, name="table_warm")
+        eps = keep.tile([P, 1], F32, name="eps")
+        row_sums = keep.tile([P, T, H], F32, name="row_sums")
+        abs_sums = keep.tile([P, T], F32, name="abs_sums")
+        row_mask = keep.tile([P, T], F32, name="row_mask")
+        o_scale = keep.tile([P, T, H], F32, name="o_scale")
+        stats = keep.tile([P, T, STAT_CHUNKS, BN_STATS_DIM], F32, name="stats")
+        mean_var = keep.tile([P, T, BN_AGGR_DIM], F32, name="mean_var")
+        std = keep.tile([P, T], F32, name="std")
+        rstd = keep.tile([P, T], F32, name="rstd")
+
+        nc.vector.memset(w_planes[:].bitcast(I32), 0)
+        nc.vector.memset(table_warm[:], 1.0)
+        nc.vector.memset(eps[:], LN_EPS)
+        nc.gpsimd.memset(bv_rows[:], 0.0)
+        masks.make_identity(nc, ident_bf[:])
+        masks.make_identity(nc, ident_f32[:])
+        nc.scalar.activation(out=table_warm[:, 1:2], in_=table_warm[:, 0:1], func=ACT.Exp)
+
+        raw_keys = {}
+
+        def load_keys_and_weights(c):
+            g0 = c * PASSES_PER_LOAD
+            raw_keys[c] = raw.tile([P, T, PASSES_PER_LOAD * K_PASS], BF16, name="raw_keys%d" % c, tag="raw")
+            nc.sync.dma_start(
+                out=raw_keys[c][:],
+                in_=keys_rows[:, :, g0 * K_PASS : (g0 + PASSES_PER_LOAD) * K_PASS],
+            )
+            if c == 0:
+                load_weight_scales()
+            nc.sync.dma_start(
+                out=w_words[:, g0 : g0 + PASSES_PER_LOAD, :].bitcast(I32),
+                in_=Wv_words[g0 : g0 + PASSES_PER_LOAD].rearrange("g p n f -> p g (n f)").bitcast(I32),
+            )
+            if c == LOADS - 1:
+                nc.sync.dma_start(out=x_sb[:], in_=x_rows)
+                nc.sync.dma_start(out=gamma_all[:], in_=ln_gamma.partition_broadcast(P))
+                nc.sync.dma_start(out=beta_all[:], in_=ln_beta.partition_broadcast(P))
+
+        def load_weight_scales():
+            for tile_index in range(G // PLANES_PER_TILE):
+                g0 = tile_index * PLANES_PER_TILE
+                for quadrant in range(4):
+                    nc.sync.dma_start(
+                        out=w_planes[32 * quadrant : 32 * quadrant + 16, tile_index, :].bitcast(I32),
+                        in_=Wv_scales[g0 : g0 + PLANES_PER_TILE, 4 * quadrant : 4 * quadrant + 4, :].bitcast(I32),
+                    )
+
+        raw_k = raw.tile([P, T, D], BF16, name="raw_k", tag="raw")
+        raw_q = raw.tile([P, T, D], BF16, name="raw_q", tag="raw")
+        for rows, tile_sb in ((k_rows, raw_k), (q_rows, raw_q)):
+            for half in range(2):
+                cols = slice(half * (D // 2), (half + 1) * (D // 2))
+                nc.sync.dma_start(out=tile_sb[:, :, cols], in_=rows[:, :, cols])
+        nc.sync.dma_start(out=bv_rows[0:H, :], in_=bv.rearrange("(h c) -> h c", c=DH))
+        load_keys_and_weights(0)
+
+        def copy_out(h, out_ap, in_ap):
+            if h % 2 == 0:
+                nc.vector.tensor_copy(out=out_ap, in_=in_ap)
+            else:
+                nc.scalar.copy(out=out_ap, in_=in_ap)
+
+        for h in range(H):
+            bank = flip_banks.tile([P, T, P], BF16, name="k_bank", tag="flip")
+            for t in range(T):
+                nc.tensor.transpose(bank[:, t, :], raw_k[:, t, h * DH : (h + 1) * DH], ident_bf[:])
+            copy_out(
+                h,
+                k_flipped[:, h, :].rearrange("d (u p e) -> d u p e", u=2, e=2),
+                bank[:].rearrange("d (u e) p -> d u p e", e=2),
+            )
+        load_keys_and_weights(1)
+        for h in range(H):
+            bank = flip_banks.tile([P, T, P], BF16, name="q_bank", tag="flip")
+            for t in range(T):
+                nc.tensor.transpose(bank[:, t, :], raw_q[:, t, h * DH : (h + 1) * DH], ident_bf[:])
+            copy_out(h, q_flipped[:, h, :, :], bank[:])
+        load_keys_and_weights(2)
+        bank = flip_banks.tile([P, P], BF16, name="bv_bank", tag="flip")
+        nc.tensor.transpose(bank[:], bv_rows[:], ident_bf[:])
+        nc.vector.tensor_copy(out=bv_cols[:], in_=bank[:, 0:H])
+
+        key_banks = {}
+        keys_grouped = {}
+        v_acc = {}
+        scores = {}
+        row_max = {}
+        exp_bias = {}
+        e_sb = {}
+        e_banks = {}
+        e_grouped = {}
+
+        def flip_keys(g):
+            chunk = raw_keys[g // PASSES_PER_LOAD]
+            first_word = (g % PASSES_PER_LOAD) * (K_PASS // 2)
+            for u in range(2):
+                key_banks[g, u] = flip_banks.tile([P, 2, 2, P], F32, name="key_bank", tag="flip")
+                for e in range(2):
+                    words = chunk[:, 2 * u + e, :].bitcast(F32)
+                    for w in range(2):
+                        nc.tensor.transpose(
+                            key_banks[g, u][:, e, w, :],
+                            words[:, first_word + w : first_word + K_PASS // 2 : 2],
+                            ident_f32[:],
+                        )
+
+        def regroup_keys(g):
+            keys_grouped[g] = stage.tile([P, S, PACK], BF16, name="keys_grouped", tag="keys_grouped", align_bytes=64)
+            words = keys_grouped[g][:].bitcast(F32)
+            for u in range(2):
+                nc.scalar.copy(
+                    out=words[:, u * (S // 2) : (u + 1) * (S // 2), :].rearrange("k (p e) w -> k p e w", e=2),
+                    in_=key_banks[g, u][:].rearrange("k e w p -> k p e w"),
+                )
+
+        def quantise_keys(g):
+            nc.vector.quantize_mx(
+                out=keys_codes[:, g, :].bitcast(FP8X4),
+                scales=keys_scales[:, g, :],
+                in_=keys_grouped[g][:].rearrange("k s f -> k (s f)"),
+            )
+
+        def value_pass(h, g):
+            if g == 0:
+                v_acc[h] = acc_banks.tile([P, S], F32, name="v_acc", tag="acc")
+            plane_start = PACK * (g % PLANES_PER_TILE)
+            nc.tensor.matmul_mx(
+                out=v_acc[h][:],
+                lhsT=w_words[:, g, h * DH : (h + 1) * DH].bitcast(FP8X4),
+                lhsT_scale=w_planes[plane_start:P, g // PLANES_PER_TILE, h * DH : (h + 1) * DH],
+                rhs=keys_codes[:, g, :].bitcast(FP8X4),
+                rhs_scale=keys_scales[:, g, :],
+                start=(g == 0),
+                stop=(g == G - 1),
+            )
+
+        def unit_of(s, a):
+            index = UNITS * s + a
+            return index // T, index % T
+
+        def score_matmul(s, a):
+            h, t = unit_of(s, a)
+            scores[s, a] = score_banks.tile([P, S], F32, name="scores", tag="score")
+            nc.tensor.matmul(
+                out=scores[s, a][:], lhsT=q_flipped[:, h, t, :], rhs=k_flipped[:, h, :], start=True, stop=True
+            )
+
+        def find_row_max(s, a):
+            row_max[s, a] = small.tile([P, 1], F32, name="row_max", tag="row_max")
+            nc.vector.tensor_reduce(out=row_max[s, a][:], in_=scores[s, a][:], axis=AXIS.X, op=ALU.max)
+
+        def make_exp_bias(s, a):
+            exp_bias[s, a] = small.tile([P, 1], F32, name="exp_bias", tag="exp_bias")
+            nc.vector.tensor_scalar_mul(out=exp_bias[s, a][:], in0=row_max[s, a][:], scalar1=-SCORE_SCALE)
+
+        def exponentials(s, a):
+            h, t = unit_of(s, a)
+            if a == 0:
+                e_sb[s] = stage.tile([P, UNITS, S], BF16, name="e_sb", tag="e_sb")
+            nc.scalar.activation(
+                out=e_sb[s][:, a, :],
+                in_=scores[s, a][:],
+                func=ACT.Exp,
+                bias=exp_bias[s, a][:],
+                scale=SCORE_SCALE,
+                accum_out=row_sums[:, t, h : h + 1],
+            )
+
+        def flip_e(s):
+            e_banks[s] = flip_banks.tile([P, UNITS, 2, P], F32, name="e_bank", tag="flip")
+            for a in range(UNITS):
+                words = e_sb[s][:, a, :].bitcast(F32)
+                for u in range(2):
+                    nc.tensor.transpose(e_banks[s][:, a, u, :], words[:, u * P : (u + 1) * P], ident_f32[:])
+
+        def regroup_e(s):
+            e_grouped[s] = stage.tile([P, UNITS, P, PACK], BF16, name="e_grouped", tag="e_grouped", align_bytes=64)
+            nc.vector.tensor_copy(
+                out=e_grouped[s][:].bitcast(F32), in_=e_banks[s][:].rearrange("j a u i -> j a i u")
+            )
+
+        def quantise_e(s):
+            h, t = unit_of(s, 0)
+            nc.vector.quantize_mx(
+                out=e_codes[:, h, t : t + UNITS, :].rearrange("j a i -> j (a i)").bitcast(FP8X4),
+                scales=e_scales[:, h, t : t + UNITS, :].rearrange("j a i -> j (a i)"),
+                in_=e_grouped[s][:].rearrange("j a i f -> j (a i f)"),
+            )
+
+        def live(index):
+            return 0 <= index < G
+
+        for s in range(G + 3):
+            if live(s - 2):
+                regroup_e(s - 2)
+            if live(s - 1):
+                regroup_keys(s - 1)
+            if live(s):
+                score_matmul(s, 0)
+            if live(s - PASS_LAG):
+                for h in range(FIRST_HEADS):
+                    value_pass(h, s - PASS_LAG)
+            if live(s):
+                score_matmul(s, 1)
+                flip_keys(s)
+            if live(s - 1):
+                flip_e(s - 1)
+            if live(s):
+                find_row_max(s, 0)
+            if live(s - 3):
+                quantise_e(s - 3)
+            if live(s):
+                make_exp_bias(s, 0)
+                exponentials(s, 0)
+                find_row_max(s, 1)
+            if live(s - 1):
+                quantise_keys(s - 1)
+            if live(s):
+                make_exp_bias(s, 1)
+                exponentials(s, 1)
+            if live(s) and s % PASSES_PER_LOAD == PASSES_PER_LOAD - 1:
+                next_load = s // PASSES_PER_LOAD + RAW_BUFS
+                if next_load < LOADS:
+                    load_keys_and_weights(next_load)
+
+        v_flipped = {}
+        v_banks = {}
+        v_grouped = {}
+
+        def relu_v(h):
+            v_flipped[h] = stage.tile([P, S], BF16, name="v_flipped", tag="v_flipped", bufs=FIRST_HEADS)
+            nc.scalar.activation(
+                out=v_flipped[h][:], in_=v_acc[h][:], func=ACT.Relu, bias=bv_cols[:, h : h + 1], scale=1.0
+            )
+
+        def flip_v(h):
+            v_banks[h] = flip_banks.tile([P, 2, DH], F32, name="v_bank", tag="flip")
+            words = v_flipped[h][:].bitcast(F32)
+            for u in range(2):
+                nc.tensor.transpose(v_banks[h][:, u, :], words[:, u * P : (u + 1) * P], ident_f32[:])
+
+        def regroup_v(h):
+            v_grouped[h] = stage.tile(
+                [P, DH, PACK], BF16, name="v_grouped", tag="v_grouped", bufs=FIRST_HEADS, align_bytes=64
+            )
+            nc.vector.tensor_copy(out=v_grouped[h][:].bitcast(F32), in_=v_banks[h][:].rearrange("j u c -> j c u"))
+
+        def quantise_v(h):
+            nc.vector.quantize_mx(
+                out=v_codes[:, h, :].bitcast(FP8X4),
+                scales=v_scales[:, h, :],
+                in_=v_grouped[h][:].rearrange("j c f -> j (c f)"),
+            )
+
+        def attend(h):
+            o_bank = score_banks.tile([P, T, DH], F32, name="o_bank", tag="score")
+            for t in range(T):
+                nc.tensor.matmul_mx(
+                    out=o_bank[:, t, :],
+                    lhsT=e_codes[:, h, t, :].bitcast(FP8X4),
+                    lhsT_scale=e_scales[:, h, t, :],
+                    rhs=v_codes[:, h, :].bitcast(FP8X4),
+                    rhs_scale=v_scales[:, h, :],
+                    start=True,
+                    stop=True,
+                )
+            cols = slice(h * DH, (h + 1) * DH)
+            for t in range(T):
+                nc.vector.scalar_tensor_tensor(
+                    out=y[:, t, cols],
+                    in0=o_bank[:, t, :],
+                    scalar=o_scale[:, t, h : h + 1],
+                    in1=x_sb[:, t, cols],
+                    op0=ALU.mult,
+                    op1=ALU.add,
+                )
+            if h % STAT_HEADS == STAT_HEADS - 1:
+                chunk = h // STAT_HEADS
+                width = STAT_HEADS * DH
+                for t in range(T):
+                    nc.vector.bn_stats(out=stats[:, t, chunk, :], in_=y[:, t, chunk * width : (chunk + 1) * width])
+
+        def make_o_scale():
+            for t in range(T):
+                unread = stage.tile([P, D], BF16, name="unread", tag="unread")
+                nc.scalar.activation(out=unread[:], in_=x_sb[:, t, :], func=ACT.Abs, accum_out=abs_sums[:, t : t + 1])
+            nc.scalar.activation(out=table_warm[:, 1:2], in_=table_warm[:, 0:1], func=ACT.Sqrt)
+            nc.vector.tensor_single_scalar(out=row_mask[:], in_=abs_sums[:], scalar=0.0, op=ALU.is_gt)
+            nc.vector.reciprocal(out=o_scale[:], in_=row_sums[:])
+            nc.vector.tensor_tensor(
+                out=o_scale[:], in0=o_scale[:], in1=row_mask[:].unsqueeze(2).to_broadcast([P, T, H]), op=ALU.mult
+            )
+
+        closed_before = []
+        for block in range(FIRST_HEADS, H + 1):
+            closed = list(range(FIRST_HEADS)) if block == FIRST_HEADS else [block - 1]
+            for h in closed:
+                relu_v(h)
+            if block < H:
+                for g in range(G):
+                    value_pass(block, g)
+            for h in closed_before:
+                attend(h)
+            for h in closed:
+                flip_v(h)
+            for h in closed:
+                regroup_v(h)
+            for h in closed:
+                quantise_v(h)
+            if block == FIRST_HEADS:
+                make_o_scale()
+            closed_before = closed
+        for h in closed_before:
+            attend(h)
+
+        for t in range(T):
+            nc.vector.bn_aggr(out=mean_var[:, t, :], in_=stats[:, t, :, :].rearrange("p c f -> p (c f)"))
+        nc.scalar.activation(
+            out=std[:], in_=mean_var[:, :, 1:2].rearrange("p t o -> p (t o)"), func=ACT.Sqrt, bias=eps[:], scale=1.0
+        )
+
+        def centre_and_gain(t):
+            nc.vector.scalar_tensor_tensor(
+                out=y[:, t, :], in0=y[:, t, :], scalar=mean_var[:, t, 0:1], in1=gamma_all[:],
+                op0=ALU.subtract, op1=ALU.mult,
+            )
+
+        def normalise_and_shift(t):
+            nc.vector.scalar_tensor_tensor(
+                out=y[:, t, :], in0=y[:, t, :], scalar=rstd[:, t : t + 1], in1=beta_all[:],
+                op0=ALU.mult, op1=ALU.add,
+            )
+
+        centre_and_gain(0)
+        centre_and_gain(1)
+        nc.vector.reciprocal(out=rstd[:], in_=std[:])
+        for t in range(T):
+            normalise_and_shift(t)
+            nc.sync.dma_start(out=out_rows[:, t, :], in_=y[:, t, :])
+            if t + 2 < T:
+                centre_and_gain(t + 2)

@@ -24,6 +24,7 @@ H = 8
 DH = D // H
 T = S // P
 G = DK // K_PASS
+UNITS = H * T
 LN_EPS = 1e-8
 SCORE_SCALE = 1.0 / math.sqrt(DH)
 
@@ -34,10 +35,13 @@ PASSES_PER_LOAD = 2
 LOADS = G // PASSES_PER_LOAD
 RAW_BUFS = 3
 FIRST_HEADS = 3
-UNITS = 2
 PASS_LAG = 2
-STAT_HEADS = 2
-STAT_CHUNKS = H // STAT_HEADS
+ROUNDS = G + PASS_LAG
+SLOT_PASSES = 4
+HEAD_SLOTS = G // SLOT_PASSES
+PER_BANK = 2
+FIRST_ATTEND_SLOT = ROUNDS + HEAD_SLOTS
+STAT_EDGES = (0, 4, 7, 8)
 BN_STATS_DIM = 6
 BN_AGGR_DIM = 2
 
@@ -67,11 +71,11 @@ def tile_multiheadattentionlayer_pa_k_kernel(
         w_planes = keep.tile([P, G // PLANES_PER_TILE, D], U8, name="w_planes", align_bytes=64)
         keys_codes = keep.tile([P, G, S], U32, name="keys_codes", align_bytes=64)
         keys_scales = keep.tile([P, G, S], U8, name="keys_scales", align_bytes=64)
-        e_codes = keep.tile([P, H, T, P], U32, name="e_codes", align_bytes=64)
-        e_scales = keep.tile([P, H, T, P], U8, name="e_scales", align_bytes=64)
+        e_codes = keep.tile([P, UNITS, P], U32, name="e_codes", align_bytes=64)
+        e_scales = keep.tile([P, UNITS, P], U8, name="e_scales", align_bytes=64)
         v_codes = keep.tile([P, H, DH], U32, name="v_codes", align_bytes=64)
         v_scales = keep.tile([P, H, DH], U8, name="v_scales", align_bytes=64)
-        q_flipped = keep.tile([P, H, T, P], BF16, name="q_flipped")
+        q_flipped = keep.tile([P, UNITS, P], BF16, name="q_flipped")
         k_flipped = keep.tile([P, H, S], BF16, name="k_flipped")
         x_sb = keep.tile([P, T, D], BF16, name="x_sb")
         y = keep.tile([P, T, D], F32, name="y")
@@ -83,14 +87,17 @@ def tile_multiheadattentionlayer_pa_k_kernel(
         bv_cols = keep.tile([P, H], F32, name="bv_cols")
         table_warm = keep.tile([P, 2], F32, name="table_warm")
         eps = keep.tile([P, 1], F32, name="eps")
-        row_sums = keep.tile([P, T, H], F32, name="row_sums")
+        row_sums = keep.tile([P, UNITS], F32, name="row_sums")
+        o_scale = keep.tile([P, UNITS], F32, name="o_scale")
+        abs_unread = keep.tile([P, D], BF16, name="abs_unread")
         abs_sums = keep.tile([P, T], F32, name="abs_sums")
         row_mask = keep.tile([P, T], F32, name="row_mask")
-        o_scale = keep.tile([P, T, H], F32, name="o_scale")
-        stats = keep.tile([P, T, STAT_CHUNKS, BN_STATS_DIM], F32, name="stats")
+        stats = keep.tile([P, T, len(STAT_EDGES) - 1, BN_STATS_DIM], F32, name="stats")
         mean_var = keep.tile([P, T, BN_AGGR_DIM], F32, name="mean_var")
+        masked_var = keep.tile([P, T], F32, name="masked_var")
         std = keep.tile([P, T], F32, name="std")
         rstd = keep.tile([P, T], F32, name="rstd")
+        out_scale = keep.tile([P, T], F32, name="out_scale")
 
         nc.vector.memset(w_planes[:].bitcast(I32), 0)
         nc.vector.memset(table_warm[:], 1.0)
@@ -101,6 +108,22 @@ def tile_multiheadattentionlayer_pa_k_kernel(
         nc.scalar.activation(out=table_warm[:, 1:2], in_=table_warm[:, 0:1], func=ACT.Exp)
 
         raw_keys = {}
+        first_cols = slice(0, FIRST_HEADS * DH)
+        other_cols = slice(FIRST_HEADS * DH, D)
+
+        def load_weights(c, cols):
+            g0 = c * PASSES_PER_LOAD
+            words = Wv_words[g0 : g0 + PASSES_PER_LOAD].rearrange("g p n f -> p g (n f)").bitcast(I32)
+            nc.sync.dma_start(out=w_words[:, g0 : g0 + PASSES_PER_LOAD, cols].bitcast(I32), in_=words[:, :, cols])
+
+        def load_weight_scales():
+            for tile_index in range(G // PLANES_PER_TILE):
+                g0 = tile_index * PLANES_PER_TILE
+                for quadrant in range(4):
+                    nc.sync.dma_start(
+                        out=w_planes[32 * quadrant : 32 * quadrant + 16, tile_index, :].bitcast(I32),
+                        in_=Wv_scales[g0 : g0 + PLANES_PER_TILE, 4 * quadrant : 4 * quadrant + 4, :].bitcast(I32),
+                    )
 
         def load_keys_and_weights(c):
             g0 = c * PASSES_PER_LOAD
@@ -111,23 +134,15 @@ def tile_multiheadattentionlayer_pa_k_kernel(
             )
             if c == 0:
                 load_weight_scales()
-            nc.sync.dma_start(
-                out=w_words[:, g0 : g0 + PASSES_PER_LOAD, :].bitcast(I32),
-                in_=Wv_words[g0 : g0 + PASSES_PER_LOAD].rearrange("g p n f -> p g (n f)").bitcast(I32),
-            )
+            load_weights(c, first_cols)
+            if c >= RAW_BUFS:
+                load_weights(c - RAW_BUFS, other_cols)
             if c == LOADS - 1:
+                for late in range(LOADS - RAW_BUFS, LOADS):
+                    load_weights(late, other_cols)
                 nc.sync.dma_start(out=x_sb[:], in_=x_rows)
                 nc.sync.dma_start(out=gamma_all[:], in_=ln_gamma.partition_broadcast(P))
                 nc.sync.dma_start(out=beta_all[:], in_=ln_beta.partition_broadcast(P))
-
-        def load_weight_scales():
-            for tile_index in range(G // PLANES_PER_TILE):
-                g0 = tile_index * PLANES_PER_TILE
-                for quadrant in range(4):
-                    nc.sync.dma_start(
-                        out=w_planes[32 * quadrant : 32 * quadrant + 16, tile_index, :].bitcast(I32),
-                        in_=Wv_scales[g0 : g0 + PLANES_PER_TILE, 4 * quadrant : 4 * quadrant + 4, :].bitcast(I32),
-                    )
 
         raw_k = raw.tile([P, T, D], BF16, name="raw_k", tag="raw")
         raw_q = raw.tile([P, T, D], BF16, name="raw_q", tag="raw")
@@ -158,7 +173,7 @@ def tile_multiheadattentionlayer_pa_k_kernel(
             bank = flip_banks.tile([P, T, P], BF16, name="q_bank", tag="flip")
             for t in range(T):
                 nc.tensor.transpose(bank[:, t, :], raw_q[:, t, h * DH : (h + 1) * DH], ident_bf[:])
-            copy_out(h, q_flipped[:, h, :, :], bank[:])
+            copy_out(h, q_flipped[:, h * T : (h + 1) * T, :], bank[:])
         load_keys_and_weights(2)
         bank = flip_banks.tile([P, P], BF16, name="bv_bank", tag="flip")
         nc.tensor.transpose(bank[:], bv_rows[:], ident_bf[:])
@@ -167,12 +182,7 @@ def tile_multiheadattentionlayer_pa_k_kernel(
         key_banks = {}
         keys_grouped = {}
         v_acc = {}
-        scores = {}
-        row_max = {}
-        exp_bias = {}
-        e_sb = {}
-        e_banks = {}
-        e_grouped = {}
+        v_flipped = {}
 
         def flip_keys(g):
             chunk = raw_keys[g // PASSES_PER_LOAD]
@@ -218,131 +228,75 @@ def tile_multiheadattentionlayer_pa_k_kernel(
                 stop=(g == G - 1),
             )
 
-        def unit_of(s, a):
-            index = UNITS * s + a
-            return index // T, index % T
-
-        def score_matmul(s, a):
-            h, t = unit_of(s, a)
-            scores[s, a] = score_banks.tile([P, S], F32, name="scores", tag="score")
-            nc.tensor.matmul(
-                out=scores[s, a][:], lhsT=q_flipped[:, h, t, :], rhs=k_flipped[:, h, :], start=True, stop=True
-            )
-
-        def find_row_max(s, a):
-            row_max[s, a] = small.tile([P, 1], F32, name="row_max", tag="row_max")
-            nc.vector.tensor_reduce(out=row_max[s, a][:], in_=scores[s, a][:], axis=AXIS.X, op=ALU.max)
-
-        def make_exp_bias(s, a):
-            exp_bias[s, a] = small.tile([P, 1], F32, name="exp_bias", tag="exp_bias")
-            nc.vector.tensor_scalar_mul(out=exp_bias[s, a][:], in0=row_max[s, a][:], scalar1=-SCORE_SCALE)
-
-        def exponentials(s, a):
-            h, t = unit_of(s, a)
-            if a == 0:
-                e_sb[s] = stage.tile([P, UNITS, S], BF16, name="e_sb", tag="e_sb")
-            nc.scalar.activation(
-                out=e_sb[s][:, a, :],
-                in_=scores[s, a][:],
-                func=ACT.Exp,
-                bias=exp_bias[s, a][:],
-                scale=SCORE_SCALE,
-                accum_out=row_sums[:, t, h : h + 1],
-            )
-
-        def flip_e(s):
-            e_banks[s] = flip_banks.tile([P, UNITS, 2, P], F32, name="e_bank", tag="flip")
-            for a in range(UNITS):
-                words = e_sb[s][:, a, :].bitcast(F32)
-                for u in range(2):
-                    nc.tensor.transpose(e_banks[s][:, a, u, :], words[:, u * P : (u + 1) * P], ident_f32[:])
-
-        def regroup_e(s):
-            e_grouped[s] = stage.tile([P, UNITS, P, PACK], BF16, name="e_grouped", tag="e_grouped", align_bytes=64)
-            nc.vector.tensor_copy(
-                out=e_grouped[s][:].bitcast(F32), in_=e_banks[s][:].rearrange("j a u i -> j a i u")
-            )
-
-        def quantise_e(s):
-            h, t = unit_of(s, 0)
-            nc.vector.quantize_mx(
-                out=e_codes[:, h, t : t + UNITS, :].rearrange("j a i -> j (a i)").bitcast(FP8X4),
-                scales=e_scales[:, h, t : t + UNITS, :].rearrange("j a i -> j (a i)"),
-                in_=e_grouped[s][:].rearrange("j a i f -> j (a i f)"),
-            )
-
-        def live(index):
-            return 0 <= index < G
-
-        for s in range(G + 3):
-            if live(s - 2):
-                regroup_e(s - 2)
-            if live(s - 1):
-                regroup_keys(s - 1)
-            if live(s):
-                score_matmul(s, 0)
-            if live(s - PASS_LAG):
-                for h in range(FIRST_HEADS):
-                    value_pass(h, s - PASS_LAG)
-            if live(s):
-                score_matmul(s, 1)
-                flip_keys(s)
-            if live(s - 1):
-                flip_e(s - 1)
-            if live(s):
-                find_row_max(s, 0)
-            if live(s - 3):
-                quantise_e(s - 3)
-            if live(s):
-                make_exp_bias(s, 0)
-                exponentials(s, 0)
-                find_row_max(s, 1)
-            if live(s - 1):
-                quantise_keys(s - 1)
-            if live(s):
-                make_exp_bias(s, 1)
-                exponentials(s, 1)
-            if live(s) and s % PASSES_PER_LOAD == PASSES_PER_LOAD - 1:
-                next_load = s // PASSES_PER_LOAD + RAW_BUFS
-                if next_load < LOADS:
-                    load_keys_and_weights(next_load)
-
-        v_flipped = {}
-        v_banks = {}
-        v_grouped = {}
-
         def relu_v(h):
-            v_flipped[h] = stage.tile([P, S], BF16, name="v_flipped", tag="v_flipped", bufs=FIRST_HEADS)
+            v_flipped[h] = stage.tile([P, S], BF16, name="v_flipped", tag="v_flipped", bufs=FIRST_HEADS + 1)
             nc.scalar.activation(
                 out=v_flipped[h][:], in_=v_acc[h][:], func=ACT.Relu, bias=bv_cols[:, h : h + 1], scale=1.0
             )
 
-        def flip_v(h):
-            v_banks[h] = flip_banks.tile([P, 2, DH], F32, name="v_bank", tag="flip")
-            words = v_flipped[h][:].bitcast(F32)
-            for u in range(2):
-                nc.tensor.transpose(v_banks[h][:, u, :], words[:, u * P : (u + 1) * P], ident_f32[:])
+        banks = {}
+        grouped = {}
 
-        def regroup_v(h):
-            v_grouped[h] = stage.tile(
-                [P, DH, PACK], BF16, name="v_grouped", tag="v_grouped", bufs=FIRST_HEADS, align_bytes=64
+        def flip(kind, rows, first, count):
+            banks[kind, first] = flip_banks.tile([P, count, 2, P], F32, name=kind + "_bank", tag="flip")
+            for a in range(count):
+                words = rows[first + a][:].bitcast(F32)
+                for u in range(2):
+                    nc.tensor.transpose(banks[kind, first][:, a, u, :], words[:, u * P : (u + 1) * P], ident_f32[:])
+
+        def regroup(copy, kind, first, count):
+            grouped[kind, first] = stage.tile(
+                [P, count, P, PACK], BF16, name=kind + "_grouped", tag=kind + "_grouped", align_bytes=64
             )
-            nc.vector.tensor_copy(out=v_grouped[h][:].bitcast(F32), in_=v_banks[h][:].rearrange("j u c -> j c u"))
+            copy(out=grouped[kind, first][:].bitcast(F32), in_=banks[kind, first][:].rearrange("j a u r -> j a r u"))
 
-        def quantise_v(h):
+        def quantise(kind, codes, scales, first, count):
             nc.vector.quantize_mx(
-                out=v_codes[:, h, :].bitcast(FP8X4),
-                scales=v_scales[:, h, :],
-                in_=v_grouped[h][:].rearrange("j c f -> j (c f)"),
+                out=codes[:, first : first + count, :].rearrange("j a r -> j (a r)").bitcast(FP8X4),
+                scales=scales[:, first : first + count, :].rearrange("j a r -> j (a r)"),
+                in_=grouped[kind, first][:].rearrange("j a r f -> j (a r f)"),
+            )
+
+        def in_banks(first, end):
+            return [(start, min(PER_BANK, end - start)) for start in range(first, end, PER_BANK)]
+
+        scores = {}
+        row_max = {}
+        exp_bias = {}
+        e_sb = {}
+
+        def score_matmul(n):
+            scores[n] = score_banks.tile([P, S], F32, name="scores", tag="score")
+            nc.tensor.matmul(
+                out=scores[n][:], lhsT=q_flipped[:, n, :], rhs=k_flipped[:, n // T, :], start=True, stop=True
+            )
+
+        def find_row_max(n):
+            row_max[n] = small.tile([P, 1], F32, name="row_max", tag="row_max")
+            nc.vector.tensor_reduce(out=row_max[n][:], in_=scores[n][:], axis=AXIS.X, op=ALU.max)
+
+        def make_exp_bias(n):
+            exp_bias[n] = small.tile([P, 1], F32, name="exp_bias", tag="exp_bias")
+            nc.vector.tensor_scalar_mul(out=exp_bias[n][:], in0=row_max[n][:], scalar1=-SCORE_SCALE)
+
+        def exponentials(n):
+            e_sb[n] = stage.tile([P, S], BF16, name="e_sb", tag="e_sb", bufs=HEAD_SLOTS + 2)
+            nc.scalar.activation(
+                out=e_sb[n][:],
+                in_=scores[n][:],
+                func=ACT.Exp,
+                bias=exp_bias[n][:],
+                scale=SCORE_SCALE,
+                accum_out=row_sums[:, n : n + 1],
             )
 
         def attend(h):
-            o_bank = score_banks.tile([P, T, DH], F32, name="o_bank", tag="score")
+            o_bank = acc_banks.tile([P, T, DH], F32, name="o_bank", tag="acc")
             for t in range(T):
                 nc.tensor.matmul_mx(
                     out=o_bank[:, t, :],
-                    lhsT=e_codes[:, h, t, :].bitcast(FP8X4),
-                    lhsT_scale=e_scales[:, h, t, :],
+                    lhsT=e_codes[:, h * T + t, :].bitcast(FP8X4),
+                    lhsT_scale=e_scales[:, h * T + t, :],
                     rhs=v_codes[:, h, :].bitcast(FP8X4),
                     rhs_scale=v_scales[:, h, :],
                     start=True,
@@ -353,55 +307,104 @@ def tile_multiheadattentionlayer_pa_k_kernel(
                 nc.vector.scalar_tensor_tensor(
                     out=y[:, t, cols],
                     in0=o_bank[:, t, :],
-                    scalar=o_scale[:, t, h : h + 1],
+                    scalar=o_scale[:, h * T + t : h * T + t + 1],
                     in1=x_sb[:, t, cols],
                     op0=ALU.mult,
                     op1=ALU.add,
                 )
-            if h % STAT_HEADS == STAT_HEADS - 1:
-                chunk = h // STAT_HEADS
-                width = STAT_HEADS * DH
-                for t in range(T):
-                    nc.vector.bn_stats(out=stats[:, t, chunk, :], in_=y[:, t, chunk * width : (chunk + 1) * width])
 
-        def make_o_scale():
+        def row_stats(chunk):
+            cols = slice(STAT_EDGES[chunk] * DH, STAT_EDGES[chunk + 1] * DH)
             for t in range(T):
-                unread = stage.tile([P, D], BF16, name="unread", tag="unread")
-                nc.scalar.activation(out=unread[:], in_=x_sb[:, t, :], func=ACT.Abs, accum_out=abs_sums[:, t : t + 1])
-            nc.scalar.activation(out=table_warm[:, 1:2], in_=table_warm[:, 0:1], func=ACT.Sqrt)
-            nc.vector.tensor_single_scalar(out=row_mask[:], in_=abs_sums[:], scalar=0.0, op=ALU.is_gt)
-            nc.vector.reciprocal(out=o_scale[:], in_=row_sums[:])
-            nc.vector.tensor_tensor(
-                out=o_scale[:], in0=o_scale[:], in1=row_mask[:].unsqueeze(2).to_broadcast([P, T, H]), op=ALU.mult
-            )
+                nc.vector.bn_stats(out=stats[:, t, chunk, :], in_=y[:, t, cols])
 
-        closed_before = []
-        for block in range(FIRST_HEADS, H + 1):
-            closed = list(range(FIRST_HEADS)) if block == FIRST_HEADS else [block - 1]
-            for h in closed:
-                relu_v(h)
-            if block < H:
-                for g in range(G):
-                    value_pass(block, g)
-            for h in closed_before:
-                attend(h)
-            for h in closed:
-                flip_v(h)
-            for h in closed:
-                regroup_v(h)
-            for h in closed:
-                quantise_v(h)
-            if block == FIRST_HEADS:
-                make_o_scale()
-            closed_before = closed
-        for h in closed_before:
-            attend(h)
+        def live(g):
+            return 0 <= g < G
+
+        for s in range(ROUNDS):
+            if live(s - 1):
+                regroup_keys(s - 1)
+            score_matmul(s)
+            if live(s - PASS_LAG):
+                for h in range(FIRST_HEADS):
+                    value_pass(h, s - PASS_LAG)
+            if s - PASS_LAG == G - 1:
+                for h in range(FIRST_HEADS):
+                    relu_v(h)
+            if live(s):
+                flip_keys(s)
+            if s >= 1:
+                flip("e", e_sb, s - 1, 1)
+            find_row_max(s)
+            if s >= 2:
+                quantise("e", e_codes, e_scales, s - 2, 1)
+            make_exp_bias(s)
+            exponentials(s)
+            if live(s - 1):
+                quantise_keys(s - 1)
+            if s >= 1:
+                regroup(nc.vector.tensor_copy, "e", s - 1, 1)
+            if live(s) and s % PASSES_PER_LOAD == PASSES_PER_LOAD - 1:
+                next_load = s // PASSES_PER_LOAD + RAW_BUFS
+                if next_load < LOADS:
+                    load_keys_and_weights(next_load)
+        to_quantise = [(ROUNDS - 2, 1)]
+
+        for head in range(FIRST_HEADS, H):
+            first_slot = ROUNDS + (head - FIRST_HEADS) * HEAD_SLOTS
+            for i in range(HEAD_SLOTS):
+                n = first_slot + i
+                if n < UNITS:
+                    score_matmul(n)
+                for g in range(i * SLOT_PASSES, (i + 1) * SLOT_PASSES):
+                    value_pass(head, g)
+                if i == HEAD_SLOTS - 1:
+                    relu_v(head)
+                if n < UNITS:
+                    find_row_max(n)
+                if i < len(to_quantise):
+                    quantise("e", e_codes, e_scales, to_quantise[i][0], to_quantise[i][1])
+                if n < UNITS:
+                    make_exp_bias(n)
+                    exponentials(n)
+                elif n < UNITS + T:
+                    t = n - UNITS
+                    nc.scalar.activation(
+                        out=abs_unread[:], in_=x_sb[:, t, :], func=ACT.Abs, accum_out=abs_sums[:, t : t + 1]
+                    )
+                elif n == UNITS + T:
+                    nc.scalar.activation(out=table_warm[:, 1:2], in_=table_warm[:, 0:1], func=ACT.Sqrt)
+                    nc.vector.tensor_single_scalar(out=row_mask[:], in_=abs_sums[:], scalar=0.0, op=ALU.is_gt)
+                attended = n - FIRST_ATTEND_SLOT
+                if attended >= 0 and attended % 2 == 0 and attended // 2 < head:
+                    attend(attended // 2)
+                if n == UNITS + 1:
+                    row_stats(0)
+                if n == UNITS + 3:
+                    row_stats(1)
+            to_quantise = in_banks(first_slot - 1, min(first_slot - 1 + HEAD_SLOTS, UNITS))
+            for first, count in to_quantise:
+                flip("e", e_sb, first, count)
+                regroup(nc.scalar.copy, "e", first, count)
+            closed = in_banks(0 if head == FIRST_HEADS else head, head + 1)
+            for first, count in closed:
+                flip("v", v_flipped, first, count)
+            for first, count in closed:
+                regroup(nc.vector.tensor_copy, "v", first, count)
+            for first, count in closed:
+                units = slice(first * T, (first + count) * T)
+                nc.vector.reciprocal(out=o_scale[:, units], in_=row_sums[:, units])
+            for first, count in closed:
+                quantise("v", v_codes, v_scales, first, count)
+        attend(H - 1)
+        row_stats(2)
 
         for t in range(T):
             nc.vector.bn_aggr(out=mean_var[:, t, :], in_=stats[:, t, :, :].rearrange("p c f -> p (c f)"))
-        nc.scalar.activation(
-            out=std[:], in_=mean_var[:, :, 1:2].rearrange("p t o -> p (t o)"), func=ACT.Sqrt, bias=eps[:], scale=1.0
+        nc.vector.tensor_tensor(
+            out=masked_var[:], in0=mean_var[:, :, 1:2].rearrange("p t o -> p (t o)"), in1=row_mask[:], op=ALU.mult
         )
+        nc.scalar.activation(out=std[:], in_=masked_var[:], func=ACT.Sqrt, bias=eps[:], scale=1.0)
 
         def centre_and_gain(t):
             nc.vector.scalar_tensor_tensor(
@@ -411,15 +414,16 @@ def tile_multiheadattentionlayer_pa_k_kernel(
 
         def normalise_and_shift(t):
             nc.vector.scalar_tensor_tensor(
-                out=y[:, t, :], in0=y[:, t, :], scalar=rstd[:, t : t + 1], in1=beta_all[:],
+                out=y[:, t, :], in0=y[:, t, :], scalar=out_scale[:, t : t + 1], in1=beta_all[:],
                 op0=ALU.mult, op1=ALU.add,
             )
 
         centre_and_gain(0)
-        centre_and_gain(1)
         nc.vector.reciprocal(out=rstd[:], in_=std[:])
+        centre_and_gain(1)
+        nc.vector.tensor_tensor(out=out_scale[:], in0=rstd[:], in1=row_mask[:], op=ALU.mult)
         for t in range(T):
-            normalise_and_shift(t)
-            nc.sync.dma_start(out=out_rows[:, t, :], in_=y[:, t, :])
             if t + 2 < T:
                 centre_and_gain(t + 2)
+            normalise_and_shift(t)
+            nc.sync.dma_start(out=out_rows[:, t, :], in_=y[:, t, :])

@@ -35,12 +35,18 @@ PASSES_PER_LOAD = 2
 LOADS = G // PASSES_PER_LOAD
 RAW_BUFS = 3
 FIRST_HEADS = 3
-PASS_LAG = 2
+PASS_LAG = 1
 ROUNDS = G + PASS_LAG
 SLOT_PASSES = 4
 HEAD_SLOTS = G // SLOT_PASSES
 PER_BANK = 2
-FIRST_ATTEND_SLOT = ROUNDS + HEAD_SLOTS
+HEAD_UNITS = 2
+HEAD_ORDER = "k0 k1 k2 k3 q0 q1 q2 q3 m0 m1 k4 k5 k6 k7 L1 r0 q4 q5 q6 q7 r1 L2 b0 f0 s1"
+SORTERS = "SVV"
+WARM_MATMULS = 8
+FLIP_EVERY = 2
+FLIP_PHASE = 0
+FLIP_BUFS = 3
 STAT_EDGES = (0, 4, 7, 8)
 BN_STATS_DIM = 6
 BN_AGGR_DIM = 2
@@ -77,7 +83,6 @@ def tile_multiheadattentionlayer_pa_k_kernel(
         v_scales = keep.tile([P, H, DH], U8, name="v_scales", align_bytes=64)
         q_flipped = keep.tile([P, UNITS, P], BF16, name="q_flipped")
         k_flipped = keep.tile([P, H, S], BF16, name="k_flipped")
-        x_sb = keep.tile([P, T, D], BF16, name="x_sb")
         y = keep.tile([P, T, D], F32, name="y")
         gamma_all = keep.tile([P, D], BF16, name="gamma_all")
         beta_all = keep.tile([P, D], BF16, name="beta_all")
@@ -86,6 +91,7 @@ def tile_multiheadattentionlayer_pa_k_kernel(
         bv_rows = keep.tile([P, P], BF16, name="bv_rows")
         bv_cols = keep.tile([P, H], F32, name="bv_cols")
         table_warm = keep.tile([P, 2], F32, name="table_warm")
+        warm = keep.tile([P, S], BF16, name="warm")
         eps = keep.tile([P, 1], F32, name="eps")
         row_sums = keep.tile([P, UNITS], F32, name="row_sums")
         o_scale = keep.tile([P, UNITS], F32, name="o_scale")
@@ -99,6 +105,7 @@ def tile_multiheadattentionlayer_pa_k_kernel(
         rstd = keep.tile([P, T], F32, name="rstd")
         out_scale = keep.tile([P, T], F32, name="out_scale")
 
+        nc.vector.memset(warm[:], 0.0)
         nc.vector.memset(w_planes[:].bitcast(I32), 0)
         nc.vector.memset(table_warm[:], 1.0)
         nc.vector.memset(eps[:], LN_EPS)
@@ -116,14 +123,13 @@ def tile_multiheadattentionlayer_pa_k_kernel(
             words = Wv_words[g0 : g0 + PASSES_PER_LOAD].rearrange("g p n f -> p g (n f)").bitcast(I32)
             nc.sync.dma_start(out=w_words[:, g0 : g0 + PASSES_PER_LOAD, cols].bitcast(I32), in_=words[:, :, cols])
 
-        def load_weight_scales():
-            for tile_index in range(G // PLANES_PER_TILE):
-                g0 = tile_index * PLANES_PER_TILE
-                for quadrant in range(4):
-                    nc.sync.dma_start(
-                        out=w_planes[32 * quadrant : 32 * quadrant + 16, tile_index, :].bitcast(I32),
-                        in_=Wv_scales[g0 : g0 + PLANES_PER_TILE, 4 * quadrant : 4 * quadrant + 4, :].bitcast(I32),
-                    )
+        def load_weight_scales(tile_index):
+            g0 = tile_index * PLANES_PER_TILE
+            for quadrant in range(4):
+                nc.sync.dma_start(
+                    out=w_planes[32 * quadrant : 32 * quadrant + 16, tile_index, :].bitcast(I32),
+                    in_=Wv_scales[g0 : g0 + PLANES_PER_TILE, 4 * quadrant : 4 * quadrant + 4, :].bitcast(I32),
+                )
 
         def load_keys_and_weights(c):
             g0 = c * PASSES_PER_LOAD
@@ -132,26 +138,35 @@ def tile_multiheadattentionlayer_pa_k_kernel(
                 out=raw_keys[c][:],
                 in_=keys_rows[:, :, g0 * K_PASS : (g0 + PASSES_PER_LOAD) * K_PASS],
             )
-            if c == 0:
-                load_weight_scales()
             load_weights(c, first_cols)
+            if c == 0:
+                load_weight_scales(0)
+            if c == 1:
+                for tile_index in range(1, G // PLANES_PER_TILE):
+                    load_weight_scales(tile_index)
             if c >= RAW_BUFS:
                 load_weights(c - RAW_BUFS, other_cols)
             if c == LOADS - 1:
                 for late in range(LOADS - RAW_BUFS, LOADS):
                     load_weights(late, other_cols)
-                nc.sync.dma_start(out=x_sb[:], in_=x_rows)
                 nc.sync.dma_start(out=gamma_all[:], in_=ln_gamma.partition_broadcast(P))
                 nc.sync.dma_start(out=beta_all[:], in_=ln_beta.partition_broadcast(P))
 
         raw_k = raw.tile([P, T, D], BF16, name="raw_k", tag="raw")
         raw_q = raw.tile([P, T, D], BF16, name="raw_q", tag="raw")
-        for rows, tile_sb in ((k_rows, raw_k), (q_rows, raw_q)):
-            for half in range(2):
-                cols = slice(half * (D // 2), (half + 1) * (D // 2))
-                nc.sync.dma_start(out=tile_sb[:, :, cols], in_=rows[:, :, cols])
+        for half in range(2):
+            cols = slice(half * (D // 2), (half + 1) * (D // 2))
+            nc.sync.dma_start(out=raw_k[:, :, cols], in_=k_rows[:, :, cols])
+            nc.sync.dma_start(out=raw_q[:, :, cols], in_=q_rows[:, :, cols])
         nc.sync.dma_start(out=bv_rows[0:H, :], in_=bv.rearrange("(h c) -> h c", c=DH))
         load_keys_and_weights(0)
+
+        head_flips = []
+
+        def head_bank(name):
+            pool, tag = ((flip_banks, "flip"), (acc_banks, "acc"))[len(head_flips) % 2]
+            head_flips.append(name)
+            return pool.tile([P, T, P], BF16, name=name, tag=tag)
 
         def copy_out(h, out_ap, in_ap):
             if h % 2 == 0:
@@ -159,8 +174,8 @@ def tile_multiheadattentionlayer_pa_k_kernel(
             else:
                 nc.scalar.copy(out=out_ap, in_=in_ap)
 
-        for h in range(H):
-            bank = flip_banks.tile([P, T, P], BF16, name="k_bank", tag="flip")
+        def flip_k(h):
+            bank = head_bank("k_bank")
             for t in range(T):
                 nc.tensor.transpose(bank[:, t, :], raw_k[:, t, h * DH : (h + 1) * DH], ident_bf[:])
             copy_out(
@@ -168,21 +183,37 @@ def tile_multiheadattentionlayer_pa_k_kernel(
                 k_flipped[:, h, :].rearrange("d (u p e) -> d u p e", u=2, e=2),
                 bank[:].rearrange("d (u e) p -> d u p e", e=2),
             )
-        load_keys_and_weights(1)
-        for h in range(H):
-            bank = flip_banks.tile([P, T, P], BF16, name="q_bank", tag="flip")
+
+        def flip_q(h):
+            bank = head_bank("q_bank")
             for t in range(T):
                 nc.tensor.transpose(bank[:, t, :], raw_q[:, t, h * DH : (h + 1) * DH], ident_bf[:])
             copy_out(h, q_flipped[:, h * T : (h + 1) * T, :], bank[:])
-        load_keys_and_weights(2)
-        bank = flip_banks.tile([P, P], BF16, name="bv_bank", tag="flip")
-        nc.tensor.transpose(bank[:], bv_rows[:], ident_bf[:])
-        nc.vector.tensor_copy(out=bv_cols[:], in_=bank[:, 0:H])
+
+        def flip_bias():
+            bank = head_bank("bv_bank")
+            nc.tensor.transpose(bank[:, 0, :], bv_rows[:], ident_bf[:])
+            nc.vector.tensor_copy(out=bv_cols[:], in_=bank[:, 0, 0:H])
 
         key_banks = {}
         keys_grouped = {}
         v_acc = {}
         v_flipped = {}
+
+        keys_sorted = {}
+
+        def sort_keys(g):
+            chunk = raw_keys[g // PASSES_PER_LOAD]
+            first_word = (g % PASSES_PER_LOAD) * (K_PASS // 2)
+            keys_sorted[g] = stage.tile([P, len(SORTERS), 2, P], F32, name="keys_sorted", tag="keys_sorted")
+            for t in range(len(SORTERS)):
+                copy = nc.vector.tensor_copy if SORTERS[t] == "V" else nc.gpsimd.tensor_copy if SORTERS[t] == "G" else nc.scalar.copy
+                copy(
+                    out=keys_sorted[g][:, t, :, :],
+                    in_=chunk[:, t, :].bitcast(F32)[:, first_word : first_word + K_PASS // 2].rearrange(
+                        "p (i w) -> p w i", w=2
+                    ),
+                )
 
         def flip_keys(g):
             chunk = raw_keys[g // PASSES_PER_LOAD]
@@ -192,11 +223,12 @@ def tile_multiheadattentionlayer_pa_k_kernel(
                 for e in range(2):
                     words = chunk[:, 2 * u + e, :].bitcast(F32)
                     for w in range(2):
-                        nc.tensor.transpose(
-                            key_banks[g, u][:, e, w, :],
-                            words[:, first_word + w : first_word + K_PASS // 2 : 2],
-                            ident_f32[:],
-                        )
+                        t = 2 * u + e
+                        if g > 0 and t < len(SORTERS):
+                            in_words = keys_sorted[g][:, t, w, :]
+                        else:
+                            in_words = words[:, first_word + w : first_word + K_PASS // 2 : 2]
+                        nc.tensor.transpose(key_banks[g, u][:, e, w, :], in_words, ident_f32[:])
 
         def regroup_keys(g):
             keys_grouped[g] = stage.tile([P, S, PACK], BF16, name="keys_grouped", tag="keys_grouped", align_bytes=64)
@@ -318,84 +350,161 @@ def tile_multiheadattentionlayer_pa_k_kernel(
             for t in range(T):
                 nc.vector.bn_stats(out=stats[:, t, chunk, :], in_=y[:, t, cols])
 
+        def warm_up(count):
+            for i in range(count):
+                bank = score_banks.tile([P, S], F32, name="warm_bank", tag="score")
+                nc.tensor.matmul(out=bank[:], lhsT=warm[:, 0:P], rhs=warm[:], start=True, stop=True)
+
+        def attention_unit(n):
+            score_matmul(n)
+            find_row_max(n)
+            make_exp_bias(n)
+            exponentials(n)
+
+        warm_up(WARM_MATMULS)
+        for step in HEAD_ORDER.split():
+            kind, arg = step[0], int(step[1:])
+            if kind == "k":
+                flip_k(arg)
+            elif kind == "q":
+                flip_q(arg)
+            elif kind == "u":
+                attention_unit(arg)
+            elif kind == "m":
+                score_matmul(arg)
+            elif kind == "r":
+                find_row_max(arg)
+                make_exp_bias(arg)
+                exponentials(arg)
+            elif kind == "w":
+                warm_up(arg)
+            elif kind == "L":
+                load_keys_and_weights(arg)
+            elif kind == "s":
+                sort_keys(arg)
+            elif kind == "f":
+                flip_keys(arg)
+            elif kind == "b":
+                flip_bias()
+
         def live(g):
             return 0 <= g < G
 
+        e_waiting = list(range(HEAD_UNITS))
+        e_regrouped = []
         for s in range(ROUNDS):
-            if live(s - 1):
-                regroup_keys(s - 1)
-            score_matmul(s)
+            if live(s):
+                regroup_keys(s)
+            n = s + HEAD_UNITS
+            score_matmul(n)
             if live(s - PASS_LAG):
                 for h in range(FIRST_HEADS):
                     value_pass(h, s - PASS_LAG)
             if s - PASS_LAG == G - 1:
                 for h in range(FIRST_HEADS):
                     relu_v(h)
+            if live(s + 1):
+                flip_keys(s + 1)
+            count = min(len(e_waiting), PER_BANK)
+            flip("e", e_sb, e_waiting[0], count)
+            find_row_max(n)
+            for e_first, e_count in e_regrouped:
+                quantise("e", e_codes, e_scales, e_first, e_count)
+            e_regrouped.clear()
+            make_exp_bias(n)
+            exponentials(n)
             if live(s):
-                flip_keys(s)
-            if s >= 1:
-                flip("e", e_sb, s - 1, 1)
-            find_row_max(s)
-            if s >= 2:
-                quantise("e", e_codes, e_scales, s - 2, 1)
-            make_exp_bias(s)
-            exponentials(s)
-            if live(s - 1):
-                quantise_keys(s - 1)
-            if s >= 1:
-                regroup(nc.vector.tensor_copy, "e", s - 1, 1)
-            if live(s) and s % PASSES_PER_LOAD == PASSES_PER_LOAD - 1:
+                quantise_keys(s)
+            if live(s + 2):
+                sort_keys(s + 2)
+            regroup(nc.vector.tensor_copy, "e", e_waiting[0], count)
+            e_regrouped.append((e_waiting[0], count))
+            e_waiting = e_waiting[count:]
+            e_waiting.append(n)
+            if live(s + 1) and s % PASSES_PER_LOAD == 0:
                 next_load = s // PASSES_PER_LOAD + RAW_BUFS
                 if next_load < LOADS:
                     load_keys_and_weights(next_load)
-        to_quantise = [(ROUNDS - 2, 1)]
+                elif next_load == LOADS:
+                    x_sb = raw.tile([P, T, D], BF16, name="x_sb", tag="raw")
+                    nc.sync.dma_start(out=x_sb[:], in_=x_rows)
 
-        for head in range(FIRST_HEADS, H):
-            first_slot = ROUNDS + (head - FIRST_HEADS) * HEAD_SLOTS
-            for i in range(HEAD_SLOTS):
-                n = first_slot + i
-                if n < UNITS:
-                    score_matmul(n)
-                for g in range(i * SLOT_PASSES, (i + 1) * SLOT_PASSES):
-                    value_pass(head, g)
-                if i == HEAD_SLOTS - 1:
-                    relu_v(head)
-                if n < UNITS:
-                    find_row_max(n)
-                if i < len(to_quantise):
-                    quantise("e", e_codes, e_scales, to_quantise[i][0], to_quantise[i][1])
-                if n < UNITS:
-                    make_exp_bias(n)
-                    exponentials(n)
-                elif n < UNITS + T:
-                    t = n - UNITS
-                    nc.scalar.activation(
-                        out=abs_unread[:], in_=x_sb[:, t, :], func=ACT.Abs, accum_out=abs_sums[:, t : t + 1]
-                    )
-                elif n == UNITS + T:
-                    nc.scalar.activation(out=table_warm[:, 1:2], in_=table_warm[:, 0:1], func=ACT.Sqrt)
-                    nc.vector.tensor_single_scalar(out=row_mask[:], in_=abs_sums[:], scalar=0.0, op=ALU.is_gt)
-                attended = n - FIRST_ATTEND_SLOT
-                if attended >= 0 and attended % 2 == 0 and attended // 2 < head:
-                    attend(attended // 2)
-                if n == UNITS + 1:
-                    row_stats(0)
-                if n == UNITS + 3:
-                    row_stats(1)
-            to_quantise = in_banks(first_slot - 1, min(first_slot - 1 + HEAD_SLOTS, UNITS))
-            for first, count in to_quantise:
-                flip("e", e_sb, first, count)
-                regroup(nc.scalar.copy, "e", first, count)
-            closed = in_banks(0 if head == FIRST_HEADS else head, head + 1)
-            for first, count in closed:
-                flip("v", v_flipped, first, count)
-            for first, count in closed:
-                regroup(nc.vector.tensor_copy, "v", first, count)
-            for first, count in closed:
-                units = slice(first * T, (first + count) * T)
-                nc.vector.reciprocal(out=o_scale[:, units], in_=row_sums[:, units])
-            for first, count in closed:
-                quantise("v", v_codes, v_scales, first, count)
+        next_unit = ROUNDS + HEAD_UNITS
+        waiting = [("e", next_unit - 1, 1, 0)]
+        waiting += [("v", h, 1, h) for h in range(FIRST_HEADS)]
+        regrouped = [("e", first, count) for first, count in e_regrouped]
+        quantised = set(("e", n) for n in range(e_regrouped[0][0]))
+        attended = 0
+        flips_done = 0
+
+        def quantise_regrouped():
+            for kind, first, count in regrouped:
+                if kind == "e":
+                    quantise("e", e_codes, e_scales, first, count)
+                else:
+                    quantise("v", v_codes, v_scales, first, count)
+                for a in range(count):
+                    quantised.add((kind, first + a))
+            regrouped.clear()
+
+        def run_of_flips(slot, vector_only=False):
+            due = [w for w in waiting if w[3] <= slot][:FLIP_BUFS]
+            for w in due:
+                waiting.remove(w)
+                kind, first, count, since = w
+                flip(kind, e_sb if kind == "e" else v_flipped, first, count)
+            for kind, first, count, since in due:
+                on_vector = vector_only or kind == "v"
+                regroup(nc.vector.tensor_copy if on_vector else nc.scalar.copy, kind, first, count)
+                regrouped.append((kind, first, count))
+                if kind == "v":
+                    units = slice(first * T, (first + count) * T)
+                    nc.vector.reciprocal(out=o_scale[:, units], in_=row_sums[:, units])
+
+        for slot in range((H - FIRST_HEADS) * HEAD_SLOTS):
+            head = FIRST_HEADS + slot // HEAD_SLOTS
+            i = slot % HEAD_SLOTS
+            n = next_unit + slot
+            if n < UNITS:
+                score_matmul(n)
+            for g in range(i * SLOT_PASSES, (i + 1) * SLOT_PASSES):
+                value_pass(head, g)
+            if i == HEAD_SLOTS - 1:
+                relu_v(head)
+                waiting.append(("v", head, 1, slot + 1))
+            if n < UNITS:
+                find_row_max(n)
+            ready = ("v", attended) in quantised and all(("e", attended * T + t) in quantised for t in range(T))
+            quantise_regrouped()
+            if n < UNITS:
+                make_exp_bias(n)
+                exponentials(n)
+                if (n - next_unit) % 2 == 1 or n == UNITS - 1:
+                    first = n - (n - next_unit) % 2
+                    waiting.append(("e", first, n - first + 1, slot + 1))
+            elif n < UNITS + T:
+                t = n - UNITS
+                nc.scalar.activation(
+                    out=abs_unread[:], in_=x_sb[:, t, :], func=ACT.Abs, accum_out=abs_sums[:, t : t + 1]
+                )
+            elif n == UNITS + T:
+                nc.scalar.activation(out=table_warm[:, 1:2], in_=table_warm[:, 0:1], func=ACT.Sqrt)
+                nc.vector.tensor_single_scalar(out=row_mask[:], in_=abs_sums[:], scalar=0.0, op=ALU.is_gt)
+            if ready:
+                attend(attended)
+                attended += 1
+                if attended in STAT_EDGES:
+                    row_stats(STAT_EDGES.index(attended) - 1)
+            if slot % FLIP_EVERY == FLIP_PHASE:
+                run_of_flips(slot)
+        slot = (H - FIRST_HEADS) * HEAD_SLOTS
+        run_of_flips(slot, True)
+        while attended < H - 1:
+            attend(attended)
+            attended += 1
+            if attended in STAT_EDGES:
+                row_stats(STAT_EDGES.index(attended) - 1)
+        quantise_regrouped()
         attend(H - 1)
         row_stats(2)
 

@@ -33,15 +33,16 @@ FLOPS = 2 * S * DK * D + 2 * (2 * H * S * S * DH)
 PLANES_PER_TILE = 4
 PASSES_PER_LOAD = 2
 LOADS = G // PASSES_PER_LOAD
-RAW_BUFS = 3
+RAW_BUFS = 5
 FIRST_HEADS = 3
+SECOND_HEADS = 5
 PASS_LAG = 1
 ROUNDS = G + PASS_LAG
 SLOT_PASSES = 4
 HEAD_SLOTS = G // SLOT_PASSES
 PER_BANK = 2
 HEAD_UNITS = 2
-HEAD_ORDER = "k0 k1 k2 k3 q0 q1 q2 q3 m0 m1 k4 k5 k6 k7 L1 r0 q4 q5 q6 q7 r1 L2 b0 f0 s1"
+HEAD_ORDER = "k0 k1 k2 k3 q0 q1 q2 q3 m0 m1 k4 k5 k6 k7 L3 r0 q4 q5 q6 q7 r1 L4 b0 f0 s1"
 SORTERS = "SVV"
 WARM_MATMULS = 8
 FLIP_EVERY = 2
@@ -83,7 +84,6 @@ def tile_multiheadattentionlayer_pa_k_kernel(
         v_scales = keep.tile([P, H, DH], U8, name="v_scales", align_bytes=64)
         q_flipped = keep.tile([P, UNITS, P], BF16, name="q_flipped")
         k_flipped = keep.tile([P, H, S], BF16, name="k_flipped")
-        y = keep.tile([P, T, D], F32, name="y")
         gamma_all = keep.tile([P, D], BF16, name="gamma_all")
         beta_all = keep.tile([P, D], BF16, name="beta_all")
         ident_bf = keep.tile([P, P], BF16, name="ident_bf")
@@ -115,8 +115,13 @@ def tile_multiheadattentionlayer_pa_k_kernel(
         nc.scalar.activation(out=table_warm[:, 1:2], in_=table_warm[:, 0:1], func=ACT.Exp)
 
         raw_keys = {}
+        y_pairs = []
+
+        def y_rows(t):
+            return y_pairs[t // 2][:, t % 2, :]
+
         first_cols = slice(0, FIRST_HEADS * DH)
-        other_cols = slice(FIRST_HEADS * DH, D)
+        other_cols = [slice(FIRST_HEADS * DH, SECOND_HEADS * DH), slice(SECOND_HEADS * DH, D)]
 
         def load_weights(c, cols):
             g0 = c * PASSES_PER_LOAD
@@ -138,17 +143,14 @@ def tile_multiheadattentionlayer_pa_k_kernel(
                 out=raw_keys[c][:],
                 in_=keys_rows[:, :, g0 * K_PASS : (g0 + PASSES_PER_LOAD) * K_PASS],
             )
-            load_weights(c, first_cols)
-            if c == 0:
-                load_weight_scales(0)
             if c == 1:
-                for tile_index in range(1, G // PLANES_PER_TILE):
+                for tile_index in range(G // PLANES_PER_TILE):
                     load_weight_scales(tile_index)
-            if c >= RAW_BUFS:
-                load_weights(c - RAW_BUFS, other_cols)
+            load_weights(c, first_cols)
             if c == LOADS - 1:
-                for late in range(LOADS - RAW_BUFS, LOADS):
-                    load_weights(late, other_cols)
+                for cols in other_cols:
+                    for late in range(LOADS):
+                        load_weights(late, cols)
                 nc.sync.dma_start(out=gamma_all[:], in_=ln_gamma.partition_broadcast(P))
                 nc.sync.dma_start(out=beta_all[:], in_=ln_beta.partition_broadcast(P))
 
@@ -159,7 +161,8 @@ def tile_multiheadattentionlayer_pa_k_kernel(
             nc.sync.dma_start(out=raw_k[:, :, cols], in_=k_rows[:, :, cols])
             nc.sync.dma_start(out=raw_q[:, :, cols], in_=q_rows[:, :, cols])
         nc.sync.dma_start(out=bv_rows[0:H, :], in_=bv.rearrange("(h c) -> h c", c=DH))
-        load_keys_and_weights(0)
+        for c in range(RAW_BUFS - 2):
+            load_keys_and_weights(c)
 
         head_flips = []
 
@@ -337,7 +340,7 @@ def tile_multiheadattentionlayer_pa_k_kernel(
             cols = slice(h * DH, (h + 1) * DH)
             for t in range(T):
                 nc.vector.scalar_tensor_tensor(
-                    out=y[:, t, cols],
+                    out=y_rows(t)[:, cols],
                     in0=o_bank[:, t, :],
                     scalar=o_scale[:, h * T + t : h * T + t + 1],
                     in1=x_sb[:, t, cols],
@@ -348,7 +351,7 @@ def tile_multiheadattentionlayer_pa_k_kernel(
         def row_stats(chunk):
             cols = slice(STAT_EDGES[chunk] * DH, STAT_EDGES[chunk + 1] * DH)
             for t in range(T):
-                nc.vector.bn_stats(out=stats[:, t, chunk, :], in_=y[:, t, cols])
+                nc.vector.bn_stats(out=stats[:, t, chunk, :], in_=y_rows(t)[:, cols])
 
         def warm_up(count):
             for i in range(count):
@@ -428,6 +431,9 @@ def tile_multiheadattentionlayer_pa_k_kernel(
                 elif next_load == LOADS:
                     x_sb = raw.tile([P, T, D], BF16, name="x_sb", tag="raw")
                     nc.sync.dma_start(out=x_sb[:], in_=x_rows)
+                elif next_load <= LOADS + T // 2:
+                    y_pair = raw.tile([P, 2, D], F32, name="y_pair", tag="raw")
+                    y_pairs.append(y_pair)
 
         next_unit = ROUNDS + HEAD_UNITS
         waiting = [("e", next_unit - 1, 1, 0)]
@@ -517,13 +523,13 @@ def tile_multiheadattentionlayer_pa_k_kernel(
 
         def centre_and_gain(t):
             nc.vector.scalar_tensor_tensor(
-                out=y[:, t, :], in0=y[:, t, :], scalar=mean_var[:, t, 0:1], in1=gamma_all[:],
+                out=y_rows(t), in0=y_rows(t), scalar=mean_var[:, t, 0:1], in1=gamma_all[:],
                 op0=ALU.subtract, op1=ALU.mult,
             )
 
         def normalise_and_shift(t):
             nc.vector.scalar_tensor_tensor(
-                out=y[:, t, :], in0=y[:, t, :], scalar=out_scale[:, t : t + 1], in1=beta_all[:],
+                out=y_rows(t), in0=y_rows(t), scalar=out_scale[:, t : t + 1], in1=beta_all[:],
                 op0=ALU.mult, op1=ALU.add,
             )
 
@@ -535,4 +541,4 @@ def tile_multiheadattentionlayer_pa_k_kernel(
             if t + 2 < T:
                 centre_and_gain(t + 2)
             normalise_and_shift(t)
-            nc.sync.dma_start(out=out_rows[:, t, :], in_=y[:, t, :])
+            nc.sync.dma_start(out=out_rows[:, t, :], in_=y_rows(t))

@@ -42,13 +42,15 @@ SLOT_PASSES = 4
 HEAD_SLOTS = G // SLOT_PASSES
 PER_BANK = 2
 HEAD_UNITS = 2
+LAST_STORED = 2
 HEAD_ORDER = "k0 k1 k2 k3 q0 q1 q2 q3 m0 m1 k4 k5 k6 k7 L3 r0 q4 q5 q6 q7 r1 L4 b0 f0 s1"
-SORTERS = "SVV"
-WARM_MATMULS = 8
+SORTERS = ""
+WARM_MATMULS = 6
 FLIP_EVERY = 2
 FLIP_PHASE = 0
 FLIP_BUFS = 3
-STAT_EDGES = (0, 4, 7, 8)
+STAT_EDGES = (0, 4, 6, 7, 8)
+STATS_PER_SLOT = 2
 BN_STATS_DIM = 6
 BN_AGGR_DIM = 2
 
@@ -103,6 +105,7 @@ def tile_multiheadattentionlayer_pa_k_kernel(
         masked_var = keep.tile([P, T], F32, name="masked_var")
         std = keep.tile([P, T], F32, name="std")
         rstd = keep.tile([P, T], F32, name="rstd")
+        shift = keep.tile([P, T], F32, name="shift")
         out_scale = keep.tile([P, T], F32, name="out_scale")
 
         nc.vector.memset(warm[:], 0.0)
@@ -348,14 +351,13 @@ def tile_multiheadattentionlayer_pa_k_kernel(
                     op1=ALU.add,
                 )
 
-        def row_stats(chunk):
+        def tile_stats(chunk, t):
             cols = slice(STAT_EDGES[chunk] * DH, STAT_EDGES[chunk + 1] * DH)
-            for t in range(T):
-                nc.vector.bn_stats(out=stats[:, t, chunk, :], in_=y_rows(t)[:, cols])
+            nc.vector.bn_stats(out=stats[:, t, chunk, :], in_=y_rows(t)[:, cols])
 
         def warm_up(count):
             for i in range(count):
-                bank = score_banks.tile([P, S], F32, name="warm_bank", tag="score")
+                bank = acc_banks.tile([P, S], F32, name="warm_bank", tag="acc")
                 nc.tensor.matmul(out=bank[:], lhsT=warm[:, 0:P], rhs=warm[:], start=True, stop=True)
 
         def attention_unit(n):
@@ -404,8 +406,7 @@ def tile_multiheadattentionlayer_pa_k_kernel(
                 for h in range(FIRST_HEADS):
                     value_pass(h, s - PASS_LAG)
             if s - PASS_LAG == G - 1:
-                for h in range(FIRST_HEADS):
-                    relu_v(h)
+                relu_v(0)
             if live(s + 1):
                 flip_keys(s + 1)
             count = min(len(e_waiting), PER_BANK)
@@ -437,10 +438,11 @@ def tile_multiheadattentionlayer_pa_k_kernel(
 
         next_unit = ROUNDS + HEAD_UNITS
         waiting = [("e", next_unit - 1, 1, 0)]
-        waiting += [("v", h, 1, h) for h in range(FIRST_HEADS)]
+        waiting += [("v", h, 1, h + 1) for h in range(FIRST_HEADS)]
         regrouped = [("e", first, count) for first, count in e_regrouped]
         quantised = set(("e", n) for n in range(e_regrouped[0][0]))
         attended = 0
+        stats_due = []
         flips_done = 0
 
         def quantise_regrouped():
@@ -485,6 +487,8 @@ def tile_multiheadattentionlayer_pa_k_kernel(
             if n < UNITS:
                 make_exp_bias(n)
                 exponentials(n)
+                if slot + 1 < FIRST_HEADS:
+                    relu_v(slot + 1)
                 if (n - next_unit) % 2 == 1 or n == UNITS - 1:
                     first = n - (n - next_unit) % 2
                     waiting.append(("e", first, n - first + 1, slot + 1))
@@ -500,7 +504,13 @@ def tile_multiheadattentionlayer_pa_k_kernel(
                 attend(attended)
                 attended += 1
                 if attended in STAT_EDGES:
-                    row_stats(STAT_EDGES.index(attended) - 1)
+                    chunk = STAT_EDGES.index(attended) - 1
+                    stats_due.extend((chunk, t) for t in range(T))
+            if n >= UNITS:
+                for due in stats_due[:STATS_PER_SLOT]:
+                    tile_stats(due[0], due[1])
+                del_count = min(STATS_PER_SLOT, len(stats_due))
+                stats_due = stats_due[del_count:]
             if slot % FLIP_EVERY == FLIP_PHASE:
                 run_of_flips(slot)
         slot = (H - FIRST_HEADS) * HEAD_SLOTS
@@ -509,10 +519,14 @@ def tile_multiheadattentionlayer_pa_k_kernel(
             attend(attended)
             attended += 1
             if attended in STAT_EDGES:
-                row_stats(STAT_EDGES.index(attended) - 1)
+                chunk = STAT_EDGES.index(attended) - 1
+                stats_due.extend((chunk, t) for t in range(T))
+        for chunk, t in stats_due:
+            tile_stats(chunk, t)
         quantise_regrouped()
         attend(H - 1)
-        row_stats(2)
+        for t in range(T):
+            tile_stats(len(STAT_EDGES) - 2, t)
 
         for t in range(T):
             nc.vector.bn_aggr(out=mean_var[:, t, :], in_=stats[:, t, :, :].rearrange("p c f -> p (c f)"))
@@ -521,24 +535,58 @@ def tile_multiheadattentionlayer_pa_k_kernel(
         )
         nc.scalar.activation(out=std[:], in_=masked_var[:], func=ACT.Sqrt, bias=eps[:], scale=1.0)
 
-        def centre_and_gain(t):
-            nc.vector.scalar_tensor_tensor(
-                out=y_rows(t), in0=y_rows(t), scalar=mean_var[:, t, 0:1], in1=gamma_all[:],
-                op0=ALU.subtract, op1=ALU.mult,
-            )
+        halves = [slice(i * S, (i + 1) * S) for i in range(D // S)]
+        gamma_banks = []
+        beta_banks = []
+        for banks_of, pool, tag, source in (
+            (gamma_banks, score_banks, "score", gamma_all),
+            (beta_banks, flip_banks, "flip", beta_all),
+        ):
+            for half in halves:
+                bank = pool.tile([P, S], F32, name="row_bank", tag=tag)
+                nc.tensor.matmul(out=bank[:], lhsT=ident_bf[:], rhs=source[:, half], start=True, stop=True)
+                banks_of.append(bank)
+
+        def centre_and_gain(t, parts=(0, 1)):
+            for i in parts:
+                half, gamma_bank = halves[i], gamma_banks[i]
+                nc.vector.scalar_tensor_tensor(
+                    out=y_rows(t)[:, half], in0=y_rows(t)[:, half], scalar=mean_var[:, t, 0:1], in1=gamma_bank[:],
+                    op0=ALU.subtract, op1=ALU.mult,
+                )
 
         def normalise_and_shift(t):
-            nc.vector.scalar_tensor_tensor(
-                out=y_rows(t), in0=y_rows(t), scalar=out_scale[:, t : t + 1], in1=beta_all[:],
-                op0=ALU.mult, op1=ALU.add,
-            )
+            for half, beta_bank in zip(halves, beta_banks):
+                nc.vector.scalar_tensor_tensor(
+                    out=y_rows(t)[:, half], in0=y_rows(t)[:, half], scalar=out_scale[:, t : t + 1], in1=beta_bank[:],
+                    op0=ALU.mult, op1=ALU.add,
+                )
+                if t == LAST_STORED:
+                    nc.sync.dma_start(out=out_rows[:, t, half], in_=y_rows(t)[:, half])
 
-        centre_and_gain(0)
+        centre_and_gain(0, (0,))
         nc.vector.reciprocal(out=rstd[:], in_=std[:])
-        centre_and_gain(1)
         nc.vector.tensor_tensor(out=out_scale[:], in0=rstd[:], in1=row_mask[:], op=ALU.mult)
-        for t in range(T):
-            if t + 2 < T:
-                centre_and_gain(t + 2)
+        nc.vector.scalar_tensor_tensor(
+            out=shift[:], in0=mean_var[:, :, 0:1].rearrange("p t o -> p (t o)"), scalar=-1.0, in1=out_scale[:],
+            op0=ALU.mult, op1=ALU.mult,
+        )
+        centre_and_gain(0, (1,))
+        last = T - 1
+        for half in halves:
+            nc.scalar.activation(
+                out=y_rows(last)[:, half], in_=y_rows(last)[:, half], func=ACT.Identity,
+                bias=shift[:, last : last + 1], scale=out_scale[:, last : last + 1],
+            )
+        for half in halves:
+            nc.gpsimd.tensor_tensor(out=y_rows(last)[:, half], in0=y_rows(last)[:, half], in1=gamma_all[:, half], op=ALU.mult)
+            nc.gpsimd.tensor_tensor(out=y_rows(last)[:, half], in0=y_rows(last)[:, half], in1=beta_all[:, half], op=ALU.add)
+        for t in range(last):
+            if t + 1 < last:
+                centre_and_gain(t + 1)
             normalise_and_shift(t)
-            nc.sync.dma_start(out=out_rows[:, t, :], in_=y_rows(t))
+            if t != LAST_STORED:
+                nc.sync.dma_start(out=out_rows[:, t, :], in_=y_rows(t))
+            if t == 1:
+                for half in halves:
+                    nc.sync.dma_start(out=out_rows[:, last, half], in_=y_rows(last)[:, half])

@@ -42,10 +42,11 @@ SLOT_PASSES = 4
 HEAD_SLOTS = G // SLOT_PASSES
 PER_BANK = 2
 HEAD_UNITS = 2
-LAST_STORED = 2
-HEAD_ORDER = "k0 k1 k2 k3 q0 q1 q2 q3 m0 m1 k4 k5 k6 k7 L3 r0 q4 q5 q6 q7 r1 L4 b0 f0 s1"
+HEAD_ORDER = "k0 k1 k2 k3 q0 q1 q2 q3 m0 m1 k4 k5 k6 k7 L3 r0 q4 q5 q6 f0 g0 r1 q7 L4 b0"
 SORTERS = ""
 WARM_MATMULS = 6
+WARM_AT = (4, 6, 13, 15, 17)
+SCALE_LOADS = {0: (0,), 2: (1, 2, 3)}
 FLIP_EVERY = 2
 FLIP_PHASE = 0
 FLIP_BUFS = 3
@@ -146,10 +147,9 @@ def tile_multiheadattentionlayer_pa_k_kernel(
                 out=raw_keys[c][:],
                 in_=keys_rows[:, :, g0 * K_PASS : (g0 + PASSES_PER_LOAD) * K_PASS],
             )
-            if c == 1:
-                for tile_index in range(G // PLANES_PER_TILE):
-                    load_weight_scales(tile_index)
             load_weights(c, first_cols)
+            for tile_index in SCALE_LOADS.get(c, ()):
+                load_weight_scales(tile_index)
             if c == LOADS - 1:
                 for cols in other_cols:
                     for late in range(LOADS):
@@ -172,7 +172,10 @@ def tile_multiheadattentionlayer_pa_k_kernel(
         def head_bank(name):
             pool, tag = ((flip_banks, "flip"), (acc_banks, "acc"))[len(head_flips) % 2]
             head_flips.append(name)
-            return pool.tile([P, T, P], BF16, name=name, tag=tag)
+            bank = pool.tile([P, T, P], BF16, name=name, tag=tag)
+            if len(head_flips) in WARM_AT:
+                nc.tensor.matmul(out=bank[:].rearrange("p t c -> p (t c)"), lhsT=warm[:, 0:P], rhs=warm[:], start=True, stop=True)
+            return bank
 
         def copy_out(h, out_ap, in_ap):
             if h % 2 == 0:
@@ -253,24 +256,38 @@ def tile_multiheadattentionlayer_pa_k_kernel(
             )
 
         def value_pass(h, g):
+            parts = 2 if h == H - 1 else 1
+            width = S // parts
             if g == 0:
-                v_acc[h] = acc_banks.tile([P, S], F32, name="v_acc", tag="acc")
+                v_acc[h] = []
+                for part in range(parts):
+                    pool, tag = ((acc_banks, "acc"), (score_banks, "score"))[part]
+                    v_bank = pool.tile([P, width], F32, name="v_bank", tag=tag)
+                    v_acc[h].append(v_bank)
             plane_start = PACK * (g % PLANES_PER_TILE)
-            nc.tensor.matmul_mx(
-                out=v_acc[h][:],
-                lhsT=w_words[:, g, h * DH : (h + 1) * DH].bitcast(FP8X4),
-                lhsT_scale=w_planes[plane_start:P, g // PLANES_PER_TILE, h * DH : (h + 1) * DH],
-                rhs=keys_codes[:, g, :].bitcast(FP8X4),
-                rhs_scale=keys_scales[:, g, :],
-                start=(g == 0),
-                stop=(g == G - 1),
-            )
+            for part in range(parts):
+                tokens = slice(part * width, (part + 1) * width)
+                nc.tensor.matmul_mx(
+                    out=v_acc[h][part][:],
+                    lhsT=w_words[:, g, h * DH : (h + 1) * DH].bitcast(FP8X4),
+                    lhsT_scale=w_planes[plane_start:P, g // PLANES_PER_TILE, h * DH : (h + 1) * DH],
+                    rhs=keys_codes[:, g, tokens].bitcast(FP8X4),
+                    rhs_scale=keys_scales[:, g, tokens],
+                    start=(g == 0),
+                    stop=(g == G - 1),
+                )
 
         def relu_v(h):
             v_flipped[h] = stage.tile([P, S], BF16, name="v_flipped", tag="v_flipped", bufs=FIRST_HEADS + 1)
+            width = S // len(v_acc[h])
             nc.scalar.activation(
-                out=v_flipped[h][:], in_=v_acc[h][:], func=ACT.Relu, bias=bv_cols[:, h : h + 1], scale=1.0
+                out=v_flipped[h][:, 0:width], in_=v_acc[h][0][:], func=ACT.Relu, bias=bv_cols[:, h : h + 1], scale=1.0
             )
+            if width < S:
+                nc.vector.tensor_scalar(
+                    out=v_flipped[h][:, width:S], in0=v_acc[h][1][:], scalar1=bv_cols[:, h : h + 1], scalar2=0.0,
+                    op0=ALU.add, op1=ALU.max,
+                )
 
         banks = {}
         grouped = {}
@@ -328,8 +345,8 @@ def tile_multiheadattentionlayer_pa_k_kernel(
                 accum_out=row_sums[:, n : n + 1],
             )
 
-        def attend(h):
-            o_bank = acc_banks.tile([P, T, DH], F32, name="o_bank", tag="acc")
+        def attend(h, pool, tag):
+            o_bank = pool.tile([P, T, DH], F32, name="o_bank", tag=tag)
             for t in range(T):
                 nc.tensor.matmul_mx(
                     out=o_bank[:, t, :],
@@ -387,6 +404,8 @@ def tile_multiheadattentionlayer_pa_k_kernel(
                 load_keys_and_weights(arg)
             elif kind == "s":
                 sort_keys(arg)
+            elif kind == "g":
+                regroup_keys(arg)
             elif kind == "f":
                 flip_keys(arg)
             elif kind == "b":
@@ -398,7 +417,7 @@ def tile_multiheadattentionlayer_pa_k_kernel(
         e_waiting = list(range(HEAD_UNITS))
         e_regrouped = []
         for s in range(ROUNDS):
-            if live(s):
+            if live(s) and s not in keys_grouped:
                 regroup_keys(s)
             n = s + HEAD_UNITS
             score_matmul(n)
@@ -501,7 +520,7 @@ def tile_multiheadattentionlayer_pa_k_kernel(
                 nc.scalar.activation(out=table_warm[:, 1:2], in_=table_warm[:, 0:1], func=ACT.Sqrt)
                 nc.vector.tensor_single_scalar(out=row_mask[:], in_=abs_sums[:], scalar=0.0, op=ALU.is_gt)
             if ready:
-                attend(attended)
+                attend(attended, flip_banks, "flip")
                 attended += 1
                 if attended in STAT_EDGES:
                     chunk = STAT_EDGES.index(attended) - 1
@@ -513,10 +532,19 @@ def tile_multiheadattentionlayer_pa_k_kernel(
                 stats_due = stats_due[del_count:]
             if slot % FLIP_EVERY == FLIP_PHASE:
                 run_of_flips(slot)
+        halves = [slice(i * S, (i + 1) * S) for i in range(D // S)]
+
+        def spread(source, i, pool, tag):
+            bank = pool.tile([P, S], F32, name="row_bank", tag=tag)
+            nc.tensor.matmul(out=bank[:], lhsT=ident_bf[:], rhs=source[:, halves[i]], start=True, stop=True)
+            return bank
+
+        gamma_banks = [spread(gamma_all, 0, score_banks, "score")]
+        beta_banks = [spread(beta_all, i, flip_banks, "flip") for i in range(2)]
         slot = (H - FIRST_HEADS) * HEAD_SLOTS
         run_of_flips(slot, True)
         while attended < H - 1:
-            attend(attended)
+            attend(attended, acc_banks, "acc")
             attended += 1
             if attended in STAT_EDGES:
                 chunk = STAT_EDGES.index(attended) - 1
@@ -524,55 +552,46 @@ def tile_multiheadattentionlayer_pa_k_kernel(
         for chunk, t in stats_due:
             tile_stats(chunk, t)
         quantise_regrouped()
-        attend(H - 1)
-        for t in range(T):
-            tile_stats(len(STAT_EDGES) - 2, t)
+        attend(H - 1, acc_banks, "acc")
+        gamma_banks.append(spread(gamma_all, 1, score_banks, "score"))
+
+        def mean_and_variance(t):
+            nc.vector.bn_aggr(out=mean_var[:, t, :], in_=stats[:, t, :, :].rearrange("p c f -> p (c f)"))
 
         for t in range(T):
-            nc.vector.bn_aggr(out=mean_var[:, t, :], in_=stats[:, t, :, :].rearrange("p c f -> p (c f)"))
+            tile_stats(len(STAT_EDGES) - 2, t)
+            if t >= 1:
+                mean_and_variance(t - 1)
+        mean_and_variance(T - 1)
         nc.vector.tensor_tensor(
             out=masked_var[:], in0=mean_var[:, :, 1:2].rearrange("p t o -> p (t o)"), in1=row_mask[:], op=ALU.mult
         )
         nc.scalar.activation(out=std[:], in_=masked_var[:], func=ACT.Sqrt, bias=eps[:], scale=1.0)
 
-        halves = [slice(i * S, (i + 1) * S) for i in range(D // S)]
-        gamma_banks = []
-        beta_banks = []
-        for banks_of, pool, tag, source in (
-            (gamma_banks, score_banks, "score", gamma_all),
-            (beta_banks, flip_banks, "flip", beta_all),
-        ):
-            for half in halves:
-                bank = pool.tile([P, S], F32, name="row_bank", tag=tag)
-                nc.tensor.matmul(out=bank[:], lhsT=ident_bf[:], rhs=source[:, half], start=True, stop=True)
-                banks_of.append(bank)
+        def centre_and_gain(t, i):
+            nc.vector.scalar_tensor_tensor(
+                out=y_rows(t)[:, halves[i]], in0=y_rows(t)[:, halves[i]], scalar=mean_var[:, t, 0:1],
+                in1=gamma_banks[i][:], op0=ALU.subtract, op1=ALU.mult,
+            )
 
-        def centre_and_gain(t, parts=(0, 1)):
-            for i in parts:
-                half, gamma_bank = halves[i], gamma_banks[i]
-                nc.vector.scalar_tensor_tensor(
-                    out=y_rows(t)[:, half], in0=y_rows(t)[:, half], scalar=mean_var[:, t, 0:1], in1=gamma_bank[:],
-                    op0=ALU.subtract, op1=ALU.mult,
-                )
+        def normalise_and_shift(t, i):
+            nc.vector.scalar_tensor_tensor(
+                out=y_rows(t)[:, halves[i]], in0=y_rows(t)[:, halves[i]], scalar=out_scale[:, t : t + 1],
+                in1=beta_banks[i][:], op0=ALU.mult, op1=ALU.add,
+            )
 
-        def normalise_and_shift(t):
-            for half, beta_bank in zip(halves, beta_banks):
-                nc.vector.scalar_tensor_tensor(
-                    out=y_rows(t)[:, half], in0=y_rows(t)[:, half], scalar=out_scale[:, t : t + 1], in1=beta_bank[:],
-                    op0=ALU.mult, op1=ALU.add,
-                )
-                if t == LAST_STORED:
-                    nc.sync.dma_start(out=out_rows[:, t, half], in_=y_rows(t)[:, half])
+        def store(t, i):
+            nc.sync.dma_start(out=out_rows[:, t, halves[i]], in_=y_rows(t)[:, halves[i]])
 
-        centre_and_gain(0, (0,))
+        last = T - 1
+        pieces = [(t, i) for t in range(last) for i in range(len(halves))]
+        centre_and_gain(*pieces[0])
         nc.vector.reciprocal(out=rstd[:], in_=std[:])
         nc.vector.tensor_tensor(out=out_scale[:], in0=rstd[:], in1=row_mask[:], op=ALU.mult)
         nc.vector.scalar_tensor_tensor(
             out=shift[:], in0=mean_var[:, :, 0:1].rearrange("p t o -> p (t o)"), scalar=-1.0, in1=out_scale[:],
             op0=ALU.mult, op1=ALU.mult,
         )
-        centre_and_gain(0, (1,))
-        last = T - 1
         for half in halves:
             nc.scalar.activation(
                 out=y_rows(last)[:, half], in_=y_rows(last)[:, half], func=ACT.Identity,
@@ -581,12 +600,11 @@ def tile_multiheadattentionlayer_pa_k_kernel(
         for half in halves:
             nc.gpsimd.tensor_tensor(out=y_rows(last)[:, half], in0=y_rows(last)[:, half], in1=gamma_all[:, half], op=ALU.mult)
             nc.gpsimd.tensor_tensor(out=y_rows(last)[:, half], in0=y_rows(last)[:, half], in1=beta_all[:, half], op=ALU.add)
-        for t in range(last):
-            if t + 1 < last:
-                centre_and_gain(t + 1)
-            normalise_and_shift(t)
-            if t != LAST_STORED:
-                nc.sync.dma_start(out=out_rows[:, t, :], in_=y_rows(t))
-            if t == 1:
-                for half in halves:
-                    nc.sync.dma_start(out=out_rows[:, last, half], in_=y_rows(last)[:, half])
+        for j in range(len(pieces)):
+            if j + 1 < len(pieces):
+                centre_and_gain(*pieces[j + 1])
+            normalise_and_shift(*pieces[j])
+            store(*pieces[j])
+            if j == 2:
+                store(last, 0)
+        store(last, 1)

@@ -47,8 +47,8 @@ SORTERS = ""
 WARM_MATMULS = 6
 WARM_AT = (4, 6, 13, 15, 17)
 SCALE_LOADS = {0: (0,), 2: (1, 2, 3)}
-FLIP_EVERY = 2
-FLIP_PHASE = 0
+FLIP_EVERY = 3
+FLIP_PHASE = 1
 FLIP_BUFS = 3
 STAT_EDGES = (0, 4, 6, 7, 8)
 STATS_PER_SLOT = 2
@@ -103,8 +103,6 @@ def tile_multiheadattentionlayer_pa_k_kernel(
         row_mask = keep.tile([P, T], F32, name="row_mask")
         stats = keep.tile([P, T, len(STAT_EDGES) - 1, BN_STATS_DIM], F32, name="stats")
         mean_var = keep.tile([P, T, BN_AGGR_DIM], F32, name="mean_var")
-        masked_var = keep.tile([P, T], F32, name="masked_var")
-        std = keep.tile([P, T], F32, name="std")
         rstd = keep.tile([P, T], F32, name="rstd")
         shift = keep.tile([P, T], F32, name="shift")
         out_scale = keep.tile([P, T], F32, name="out_scale")
@@ -517,7 +515,7 @@ def tile_multiheadattentionlayer_pa_k_kernel(
                     out=abs_unread[:], in_=x_sb[:, t, :], func=ACT.Abs, accum_out=abs_sums[:, t : t + 1]
                 )
             elif n == UNITS + T:
-                nc.scalar.activation(out=table_warm[:, 1:2], in_=table_warm[:, 0:1], func=ACT.Sqrt)
+                nc.scalar.activation(out=table_warm[:, 1:2], in_=table_warm[:, 0:1], func=ACT.Abs_reciprocal_sqrt)
                 nc.vector.tensor_single_scalar(out=row_mask[:], in_=abs_sums[:], scalar=0.0, op=ALU.is_gt)
             if ready:
                 attend(attended, flip_banks, "flip")
@@ -563,10 +561,10 @@ def tile_multiheadattentionlayer_pa_k_kernel(
             if t >= 1:
                 mean_and_variance(t - 1)
         mean_and_variance(T - 1)
-        nc.vector.tensor_tensor(
-            out=masked_var[:], in0=mean_var[:, :, 1:2].rearrange("p t o -> p (t o)"), in1=row_mask[:], op=ALU.mult
+        nc.scalar.activation(
+            out=rstd[:], in_=mean_var[:, :, 1:2].rearrange("p t o -> p (t o)"), func=ACT.Abs_reciprocal_sqrt,
+            bias=eps[:], scale=1.0,
         )
-        nc.scalar.activation(out=std[:], in_=masked_var[:], func=ACT.Sqrt, bias=eps[:], scale=1.0)
 
         def centre_and_gain(t, i):
             nc.vector.scalar_tensor_tensor(
@@ -586,7 +584,6 @@ def tile_multiheadattentionlayer_pa_k_kernel(
         last = T - 1
         pieces = [(t, i) for t in range(last) for i in range(len(halves))]
         centre_and_gain(*pieces[0])
-        nc.vector.reciprocal(out=rstd[:], in_=std[:])
         nc.vector.tensor_tensor(out=out_scale[:], in0=rstd[:], in1=row_mask[:], op=ALU.mult)
         nc.vector.scalar_tensor_tensor(
             out=shift[:], in0=mean_var[:, :, 0:1].rearrange("p t o -> p (t o)"), scalar=-1.0, in1=out_scale[:],

@@ -36,6 +36,8 @@ LOADS = G // PASSES_PER_LOAD
 RAW_BUFS = 5
 FIRST_HEADS = 3
 SECOND_HEADS = 5
+LAST = T - 1
+TILE_ORDER = (LAST, 0, 1, 2)
 PASS_LAG = 1
 ROUNDS = G + PASS_LAG
 SLOT_PASSES = 4
@@ -43,12 +45,11 @@ HEAD_SLOTS = G // SLOT_PASSES
 PER_BANK = 2
 HEAD_UNITS = 2
 HEAD_ORDER = "k0 k1 k2 k3 q0 q1 q2 q3 m0 m1 k4 k5 k6 k7 L3 r0 q4 q5 q6 f0 g0 r1 q7 L4 b0"
-SORTERS = ""
 WARM_MATMULS = 6
 WARM_AT = (4, 6, 13, 15, 17)
 SCALE_LOADS = {0: (0,), 2: (1, 2, 3)}
-FLIP_EVERY = 3
-FLIP_PHASE = 1
+FLIP_EVERY = 1
+FLIP_PHASE = 0
 FLIP_BUFS = 3
 STAT_EDGES = (0, 4, 6, 7, 8)
 STATS_PER_SLOT = 2
@@ -104,7 +105,7 @@ def tile_multiheadattentionlayer_pa_k_kernel(
         stats = keep.tile([P, T, len(STAT_EDGES) - 1, BN_STATS_DIM], F32, name="stats")
         mean_var = keep.tile([P, T, BN_AGGR_DIM], F32, name="mean_var")
         rstd = keep.tile([P, T], F32, name="rstd")
-        shift = keep.tile([P, T], F32, name="shift")
+        minus_mean = keep.tile([P, 1], F32, name="minus_mean")
         out_scale = keep.tile([P, T], F32, name="out_scale")
 
         nc.vector.memset(warm[:], 0.0)
@@ -207,21 +208,6 @@ def tile_multiheadattentionlayer_pa_k_kernel(
         v_acc = {}
         v_flipped = {}
 
-        keys_sorted = {}
-
-        def sort_keys(g):
-            chunk = raw_keys[g // PASSES_PER_LOAD]
-            first_word = (g % PASSES_PER_LOAD) * (K_PASS // 2)
-            keys_sorted[g] = stage.tile([P, len(SORTERS), 2, P], F32, name="keys_sorted", tag="keys_sorted")
-            for t in range(len(SORTERS)):
-                copy = nc.vector.tensor_copy if SORTERS[t] == "V" else nc.gpsimd.tensor_copy if SORTERS[t] == "G" else nc.scalar.copy
-                copy(
-                    out=keys_sorted[g][:, t, :, :],
-                    in_=chunk[:, t, :].bitcast(F32)[:, first_word : first_word + K_PASS // 2].rearrange(
-                        "p (i w) -> p w i", w=2
-                    ),
-                )
-
         def flip_keys(g):
             chunk = raw_keys[g // PASSES_PER_LOAD]
             first_word = (g % PASSES_PER_LOAD) * (K_PASS // 2)
@@ -230,12 +216,11 @@ def tile_multiheadattentionlayer_pa_k_kernel(
                 for e in range(2):
                     words = chunk[:, 2 * u + e, :].bitcast(F32)
                     for w in range(2):
-                        t = 2 * u + e
-                        if g > 0 and t < len(SORTERS):
-                            in_words = keys_sorted[g][:, t, w, :]
-                        else:
-                            in_words = words[:, first_word + w : first_word + K_PASS // 2 : 2]
-                        nc.tensor.transpose(key_banks[g, u][:, e, w, :], in_words, ident_f32[:])
+                        nc.tensor.transpose(
+                            key_banks[g, u][:, e, w, :],
+                            words[:, first_word + w : first_word + K_PASS // 2 : 2],
+                            ident_f32[:],
+                        )
 
         def regroup_keys(g):
             keys_grouped[g] = stage.tile([P, S, PACK], BF16, name="keys_grouped", tag="keys_grouped", align_bytes=64)
@@ -356,7 +341,7 @@ def tile_multiheadattentionlayer_pa_k_kernel(
                     stop=True,
                 )
             cols = slice(h * DH, (h + 1) * DH)
-            for t in range(T):
+            for t in TILE_ORDER:
                 nc.vector.scalar_tensor_tensor(
                     out=y_rows(t)[:, cols],
                     in0=o_bank[:, t, :],
@@ -400,8 +385,6 @@ def tile_multiheadattentionlayer_pa_k_kernel(
                 warm_up(arg)
             elif kind == "L":
                 load_keys_and_weights(arg)
-            elif kind == "s":
-                sort_keys(arg)
             elif kind == "g":
                 regroup_keys(arg)
             elif kind == "f":
@@ -436,8 +419,6 @@ def tile_multiheadattentionlayer_pa_k_kernel(
             exponentials(n)
             if live(s):
                 quantise_keys(s)
-            if live(s + 2):
-                sort_keys(s + 2)
             regroup(nc.vector.tensor_copy, "e", e_waiting[0], count)
             e_regrouped.append((e_waiting[0], count))
             e_waiting = e_waiting[count:]
@@ -556,15 +537,13 @@ def tile_multiheadattentionlayer_pa_k_kernel(
         def mean_and_variance(t):
             nc.vector.bn_aggr(out=mean_var[:, t, :], in_=stats[:, t, :, :].rearrange("p c f -> p (c f)"))
 
-        for t in range(T):
-            tile_stats(len(STAT_EDGES) - 2, t)
-            if t >= 1:
-                mean_and_variance(t - 1)
-        mean_and_variance(T - 1)
-        nc.scalar.activation(
-            out=rstd[:], in_=mean_var[:, :, 1:2].rearrange("p t o -> p (t o)"), func=ACT.Abs_reciprocal_sqrt,
-            bias=eps[:], scale=1.0,
-        )
+        for i in range(T):
+            tile_stats(len(STAT_EDGES) - 2, TILE_ORDER[i])
+            if i >= 1:
+                mean_and_variance(TILE_ORDER[i - 1])
+            if i == 2:
+                nc.vector.tensor_scalar_mul(out=minus_mean[:], in0=mean_var[:, LAST, 0:1], scalar1=-1.0)
+        mean_and_variance(TILE_ORDER[T - 1])
 
         def centre_and_gain(t, i):
             nc.vector.scalar_tensor_tensor(
@@ -578,30 +557,42 @@ def tile_multiheadattentionlayer_pa_k_kernel(
                 in1=beta_banks[i][:], op0=ALU.mult, op1=ALU.add,
             )
 
+        def scalar_centre(i):
+            nc.scalar.activation(
+                out=y_rows(LAST)[:, halves[i]], in_=y_rows(LAST)[:, halves[i]], func=ACT.Identity, bias=minus_mean[:],
+                scale=1.0,
+            )
+
+        def scalar_normalise(t, i):
+            nc.scalar.activation(
+                out=y_rows(t)[:, halves[i]], in_=y_rows(t)[:, halves[i]], func=ACT.Copy, scale=out_scale[:, t : t + 1]
+            )
+
+        def gpsimd_row(t, i, row, op):
+            nc.gpsimd.tensor_tensor(out=y_rows(t)[:, halves[i]], in0=y_rows(t)[:, halves[i]], in1=row[:, halves[i]], op=op)
+
         def store(t, i):
             nc.sync.dma_start(out=out_rows[:, t, halves[i]], in_=y_rows(t)[:, halves[i]])
 
-        last = T - 1
-        pieces = [(t, i) for t in range(last) for i in range(len(halves))]
-        centre_and_gain(*pieces[0])
-        nc.vector.tensor_tensor(out=out_scale[:], in0=rstd[:], in1=row_mask[:], op=ALU.mult)
-        nc.vector.scalar_tensor_tensor(
-            out=shift[:], in0=mean_var[:, :, 0:1].rearrange("p t o -> p (t o)"), scalar=-1.0, in1=out_scale[:],
-            op0=ALU.mult, op1=ALU.mult,
+        scalar_centre(0)
+        nc.scalar.activation(
+            out=rstd[:], in_=mean_var[:, :, 1:2].rearrange("p t o -> p (t o)"), func=ACT.Abs_reciprocal_sqrt,
+            bias=eps[:], scale=1.0,
         )
-        for half in halves:
-            nc.scalar.activation(
-                out=y_rows(last)[:, half], in_=y_rows(last)[:, half], func=ACT.Identity,
-                bias=shift[:, last : last + 1], scale=out_scale[:, last : last + 1],
-            )
-        for half in halves:
-            nc.gpsimd.tensor_tensor(out=y_rows(last)[:, half], in0=y_rows(last)[:, half], in1=gamma_all[:, half], op=ALU.mult)
-            nc.gpsimd.tensor_tensor(out=y_rows(last)[:, half], in0=y_rows(last)[:, half], in1=beta_all[:, half], op=ALU.add)
+        scalar_centre(1)
+        for i in range(2):
+            gpsimd_row(LAST, i, gamma_all, ALU.mult)
+        centre_and_gain(0, 0)
+        nc.vector.tensor_tensor(out=out_scale[:], in0=rstd[:], in1=row_mask[:], op=ALU.mult)
+        pieces = [(t, i) for t in range(LAST) for i in range(2)]
+        for i in range(2):
+            scalar_normalise(LAST, i)
+        for i in range(2):
+            gpsimd_row(LAST, i, beta_all, ALU.add)
         for j in range(len(pieces)):
             if j + 1 < len(pieces):
                 centre_and_gain(*pieces[j + 1])
             normalise_and_shift(*pieces[j])
             store(*pieces[j])
-            if j == 2:
-                store(last, 0)
-        store(last, 1)
+            if j in (2, 3):
+                store(LAST, j - 2)

from contextlib import ExitStack
import math

import concourse.masks as masks
import concourse.mybir as mybir

F32 = mybir.dt.float32
BF16 = mybir.dt.bfloat16
I32 = mybir.dt.int32
U32 = mybir.dt.uint32
U8 = mybir.dt.uint8
FP8X4 = mybir.dt.float8_e4m3fn_x4
ACT = mybir.ActivationFunctionType
ALU = mybir.AluOpType
AXIS = mybir.AxisListType

P = 128
PACK = 4
K_PASS = P * PACK
S = 512
D = 1024
DK = 8192
H = 8
DH = D // H
T = S // P
G = DK // K_PASS
UNITS = H * T
LN_EPS = 1e-8
SCORE_SCALE = 1.0 / math.sqrt(DH)

FLOPS = 2 * S * DK * D + 2 * (2 * H * S * S * DH)

PLANES_PER_TILE = 4
PASSES_PER_LOAD = 2
LOADS = G // PASSES_PER_LOAD
RAW_BUFS = 5
FIRST_HEADS = 3
SECOND_HEADS = 5
LAST = T - 1
TILE_ORDER = (LAST, 0, 1, 2)
PASS_LAG = 1
ROUNDS = G + PASS_LAG
SLOT_PASSES = 4
HEAD_SLOTS = G // SLOT_PASSES
PER_BANK = 2
HEAD_UNITS = 2
HEAD_ORDER = "k0 k1 k2 k3 q0 q1 q2 q3 m0 m1 k4 k5 k6 k7 L3 r0 q4 q5 q6 f0 g0 r1 q7 L4 b0"
WARM_MATMULS = 6
WARM_AT = (4, 6, 13, 15, 17)
SCALE_LOADS = {0: (0,), 2: (1, 2, 3)}
FLIP_EVERY = 1
FLIP_PHASE = 0
FLIP_BUFS = 3
STAT_EDGES = (0, 4, 6, 7, 8)
STATS_PER_SLOT = 2
BN_STATS_DIM = 6
BN_AGGR_DIM = 2


def tile_multiheadattentionlayer_pa_k_kernel(
    tc, q_relu, k_relu, keys, Wv_words, Wv_scales, bv, queries, ln_gamma, ln_beta, out
):
    nc = tc.nc

    q_rows = q_relu.flatten_outer_dims().rearrange("(p t) d -> p t d", t=T)
    k_rows = k_relu.flatten_outer_dims().rearrange("(p t) d -> p t d", t=T)
    x_rows = queries.flatten_outer_dims().rearrange("(p t) d -> p t d", t=T)
    keys_rows = keys.flatten_outer_dims().rearrange("(p t) k -> p t k", t=T)
    out_rows = out.flatten_outer_dims().rearrange("(p t) d -> p t d", t=T)

    with ExitStack() as ctx:
        ctx.enter_context(tc.manual_schedule())
        keep = ctx.enter_context(tc.tile_pool(name="keep", bufs=1))
        raw = ctx.enter_context(tc.tile_pool(name="raw", bufs=RAW_BUFS))
        stage = ctx.enter_context(tc.tile_pool(name="stage", bufs=2))
        small = ctx.enter_context(tc.tile_pool(name="small", bufs=4))
        acc_banks = ctx.enter_context(tc.psum_pool(name="acc_banks", bufs=FIRST_HEADS))
        score_banks = ctx.enter_context(tc.psum_pool(name="score_banks", bufs=2))
        flip_banks = ctx.enter_context(tc.psum_pool(name="flip_banks", bufs=3))

        w_words = keep.tile([P, G, D], U32, name="w_words", align_bytes=64)
        w_planes = keep.tile([P, G // PLANES_PER_TILE, D], U8, name="w_planes", align_bytes=64)
        keys_codes = keep.tile([P, G, S], U32, name="keys_codes", align_bytes=64)
        keys_scales = keep.tile([P, G, S], U8, name="keys_scales", align_bytes=64)
        e_codes = keep.tile([P, UNITS, P], U32, name="e_codes", align_bytes=64)
        e_scales = keep.tile([P, UNITS, P], U8, name="e_scales", align_bytes=64)
        v_codes = keep.tile([P, H, DH], U32, name="v_codes", align_bytes=64)
        v_scales = keep.tile([P, H, DH], U8, name="v_scales", align_bytes=64)
        q_flipped = keep.tile([P, UNITS, P], BF16, name="q_flipped")
        k_flipped = keep.tile([P, H, S], BF16, name="k_flipped")
        gamma_all = keep.tile([P, D], BF16, name="gamma_all")
        beta_all = keep.tile([P, D], BF16, name="beta_all")
        ident_bf = keep.tile([P, P], BF16, name="ident_bf")
        ident_f32 = keep.tile([P, P], F32, name="ident_f32")
        bv_rows = keep.tile([P, P], BF16, name="bv_rows")
        bv_cols = keep.tile([P, H], F32, name="bv_cols")
        table_warm = keep.tile([P, 2], F32, name="table_warm")
        warm = keep.tile([P, S], BF16, name="warm")
        eps = keep.tile([P, 1], F32, name="eps")
        row_sums = keep.tile([P, UNITS], F32, name="row_sums")
        o_scale = keep.tile([P, UNITS], F32, name="o_scale")
        abs_unread = keep.tile([P, D], BF16, name="abs_unread")
        abs_sums = keep.tile([P, T], F32, name="abs_sums")
        row_mask = keep.tile([P, T], F32, name="row_mask")
        stats = keep.tile([P, T, len(STAT_EDGES) - 1, BN_STATS_DIM], F32, name="stats")
        mean_var = keep.tile([P, T, BN_AGGR_DIM], F32, name="mean_var")
        rstd = keep.tile([P, T], F32, name="rstd")
        minus_mean = keep.tile([P, 1], F32, name="minus_mean")
        out_scale = keep.tile([P, T], F32, name="out_scale")

        nc.vector.memset(warm[:], 0.0)
        nc.vector.memset(w_planes[:].bitcast(I32), 0)
        nc.vector.memset(table_warm[:], 1.0)
        nc.vector.memset(eps[:], LN_EPS)
        nc.gpsimd.memset(bv_rows[:], 0.0)
        masks.make_identity(nc, ident_bf[:])
        masks.make_identity(nc, ident_f32[:])
        nc.scalar.activation(out=table_warm[:, 1:2], in_=table_warm[:, 0:1], func=ACT.Exp)

        raw_keys = {}
        y_pairs = []

        def y_rows(t):
            return y_pairs[t // 2][:, t % 2, :]

        first_cols = slice(0, FIRST_HEADS * DH)
        other_cols = [slice(FIRST_HEADS * DH, SECOND_HEADS * DH), slice(SECOND_HEADS * DH, D)]

        def load_weights(c, cols):
            g0 = c * PASSES_PER_LOAD
            words = Wv_words[g0 : g0 + PASSES_PER_LOAD].rearrange("g p n f -> p g (n f)").bitcast(I32)
            nc.sync.dma_start(out=w_words[:, g0 : g0 + PASSES_PER_LOAD, cols].bitcast(I32), in_=words[:, :, cols])

        def load_weight_scales(tile_index):
            g0 = tile_index * PLANES_PER_TILE
            for quadrant in range(4):
                nc.sync.dma_start(
                    out=w_planes[32 * quadrant : 32 * quadrant + 16, tile_index, :].bitcast(I32),
                    in_=Wv_scales[g0 : g0 + PLANES_PER_TILE, 4 * quadrant : 4 * quadrant + 4, :].bitcast(I32),
                )

        def load_keys_and_weights(c):
            g0 = c * PASSES_PER_LOAD
            raw_keys[c] = raw.tile([P, T, PASSES_PER_LOAD * K_PASS], BF16, name="raw_keys%d" % c, tag="raw")
            nc.sync.dma_start(
                out=raw_keys[c][:],
                in_=keys_rows[:, :, g0 * K_PASS : (g0 + PASSES_PER_LOAD) * K_PASS],
            )
            load_weights(c, first_cols)
            for tile_index in SCALE_LOADS.get(c, ()):
                load_weight_scales(tile_index)
            if c == LOADS - 1:
                for cols in other_cols:
                    for late in range(LOADS):
                        load_weights(late, cols)
                nc.sync.dma_start(out=gamma_all[:], in_=ln_gamma.partition_broadcast(P))
                nc.sync.dma_start(out=beta_all[:], in_=ln_beta.partition_broadcast(P))

        raw_k = raw.tile([P, T, D], BF16, name="raw_k", tag="raw")
        raw_q = raw.tile([P, T, D], BF16, name="raw_q", tag="raw")
        for half in range(2):
            cols = slice(half * (D // 2), (half + 1) * (D // 2))
            nc.sync.dma_start(out=raw_k[:, :, cols], in_=k_rows[:, :, cols])
            nc.sync.dma_start(out=raw_q[:, :, cols], in_=q_rows[:, :, cols])
        nc.sync.dma_start(out=bv_rows[0:H, :], in_=bv.rearrange("(h c) -> h c", c=DH))
        for c in range(RAW_BUFS - 2):
            load_keys_and_weights(c)

        head_flips = []

        def head_bank(name):
            pool, tag = ((flip_banks, "flip"), (acc_banks, "acc"))[len(head_flips) % 2]
            head_flips.append(name)
            bank = pool.tile([P, T, P], BF16, name=name, tag=tag)
            if len(head_flips) in WARM_AT:
                nc.tensor.matmul(out=bank[:].rearrange("p t c -> p (t c)"), lhsT=warm[:, 0:P], rhs=warm[:], start=True, stop=True)
            return bank

        def copy_out(h, out_ap, in_ap):
            if h % 2 == 0:
                nc.vector.tensor_copy(out=out_ap, in_=in_ap)
            else:
                nc.scalar.copy(out=out_ap, in_=in_ap)

        def flip_k(h):
            bank = head_bank("k_bank")
            for t in range(T):
                nc.tensor.transpose(bank[:, t, :], raw_k[:, t, h * DH : (h + 1) * DH], ident_bf[:])
            copy_out(
                h,
                k_flipped[:, h, :].rearrange("d (u p e) -> d u p e", u=2, e=2),
                bank[:].rearrange("d (u e) p -> d u p e", e=2),
            )

        def flip_q(h):
            bank = head_bank("q_bank")
            for t in range(T):
                nc.tensor.transpose(bank[:, t, :], raw_q[:, t, h * DH : (h + 1) * DH], ident_bf[:])
            copy_out(h, q_flipped[:, h * T : (h + 1) * T, :], bank[:])

        def flip_bias():
            bank = head_bank("bv_bank")
            nc.tensor.transpose(bank[:, 0, :], bv_rows[:], ident_bf[:])
            nc.vector.tensor_copy(out=bv_cols[:], in_=bank[:, 0, 0:H])

        key_banks = {}
        keys_grouped = {}
        v_acc = {}
        v_flipped = {}

        def flip_keys(g):
            chunk = raw_keys[g // PASSES_PER_LOAD]
            first_word = (g % PASSES_PER_LOAD) * (K_PASS // 2)
            for u in range(2):
                key_banks[g, u] = flip_banks.tile([P, 2, 2, P], F32, name="key_bank", tag="flip")
                for e in range(2):
                    words = chunk[:, 2 * u + e, :].bitcast(F32)
                    for w in range(2):
                        nc.tensor.transpose(
                            key_banks[g, u][:, e, w, :],
                            words[:, first_word + w : first_word + K_PASS // 2 : 2],
                            ident_f32[:],
                        )

        def regroup_keys(g):
            keys_grouped[g] = stage.tile([P, S, PACK], BF16, name="keys_grouped", tag="keys_grouped", align_bytes=64)
            words = keys_grouped[g][:].bitcast(F32)
            for u in range(2):
                nc.scalar.copy(
                    out=words[:, u * (S // 2) : (u + 1) * (S // 2), :].rearrange("k (p e) w -> k p e w", e=2),
                    in_=key_banks[g, u][:].rearrange("k e w p -> k p e w"),
                )

        def quantise_keys(g):
            nc.vector.quantize_mx(
                out=keys_codes[:, g, :].bitcast(FP8X4),
                scales=keys_scales[:, g, :],
                in_=keys_grouped[g][:].rearrange("k s f -> k (s f)"),
            )

        def value_pass(h, g):
            parts = 2 if h == H - 1 else 1
            width = S // parts
            if g == 0:
                v_acc[h] = []
                for part in range(parts):
                    pool, tag = ((acc_banks, "acc"), (score_banks, "score"))[part]
                    v_bank = pool.tile([P, width], F32, name="v_bank", tag=tag)
                    v_acc[h].append(v_bank)
            plane_start = PACK * (g % PLANES_PER_TILE)
            for part in range(parts):
                tokens = slice(part * width, (part + 1) * width)
                nc.tensor.matmul_mx(
                    out=v_acc[h][part][:],
                    lhsT=w_words[:, g, h * DH : (h + 1) * DH].bitcast(FP8X4),
                    lhsT_scale=w_planes[plane_start:P, g // PLANES_PER_TILE, h * DH : (h + 1) * DH],
                    rhs=keys_codes[:, g, tokens].bitcast(FP8X4),
                    rhs_scale=keys_scales[:, g, tokens],
                    start=(g == 0),
                    stop=(g == G - 1),
                )

        def relu_v(h):
            v_flipped[h] = stage.tile([P, S], BF16, name="v_flipped", tag="v_flipped", bufs=FIRST_HEADS + 1)
            width = S // len(v_acc[h])
            nc.scalar.activation(
                out=v_flipped[h][:, 0:width], in_=v_acc[h][0][:], func=ACT.Relu, bias=bv_cols[:, h : h + 1], scale=1.0
            )
            if width < S:
                nc.vector.tensor_scalar(
                    out=v_flipped[h][:, width:S], in0=v_acc[h][1][:], scalar1=bv_cols[:, h : h + 1], scalar2=0.0,
                    op0=ALU.add, op1=ALU.max,
                )

        banks = {}
        grouped = {}

        def flip(kind, rows, first, count):
            banks[kind, first] = flip_banks.tile([P, count, 2, P], F32, name=kind + "_bank", tag="flip")
            for a in range(count):
                words = rows[first + a][:].bitcast(F32)
                for u in range(2):
                    nc.tensor.transpose(banks[kind, first][:, a, u, :], words[:, u * P : (u + 1) * P], ident_f32[:])

        def regroup(copy, kind, first, count):
            grouped[kind, first] = stage.tile(
                [P, count, P, PACK], BF16, name=kind + "_grouped", tag=kind + "_grouped", align_bytes=64
            )
            copy(out=grouped[kind, first][:].bitcast(F32), in_=banks[kind, first][:].rearrange("j a u r -> j a r u"))

        def quantise(kind, codes, scales, first, count):
            nc.vector.quantize_mx(
                out=codes[:, first : first + count, :].rearrange("j a r -> j (a r)").bitcast(FP8X4),
                scales=scales[:, first : first + count, :].rearrange("j a r -> j (a r)"),
                in_=grouped[kind, first][:].rearrange("j a r f -> j (a r f)"),
            )

        def in_banks(first, end):
            return [(start, min(PER_BANK, end - start)) for start in range(first, end, PER_BANK)]

        scores = {}
        row_max = {}
        exp_bias = {}
        e_sb = {}

        def score_matmul(n):
            scores[n] = score_banks.tile([P, S], F32, name="scores", tag="score")
            nc.tensor.matmul(
                out=scores[n][:], lhsT=q_flipped[:, n, :], rhs=k_flipped[:, n // T, :], start=True, stop=True
            )

        def find_row_max(n):
            row_max[n] = small.tile([P, 1], F32, name="row_max", tag="row_max")
            nc.vector.tensor_reduce(out=row_max[n][:], in_=scores[n][:], axis=AXIS.X, op=ALU.max)

        def make_exp_bias(n):
            exp_bias[n] = small.tile([P, 1], F32, name="exp_bias", tag="exp_bias")
            nc.vector.tensor_scalar_mul(out=exp_bias[n][:], in0=row_max[n][:], scalar1=-SCORE_SCALE)

        def exponentials(n):
            e_sb[n] = stage.tile([P, S], BF16, name="e_sb", tag="e_sb", bufs=HEAD_SLOTS + 2)
            nc.scalar.activation(
                out=e_sb[n][:],
                in_=scores[n][:],
                func=ACT.Exp,
                bias=exp_bias[n][:],
                scale=SCORE_SCALE,
                accum_out=row_sums[:, n : n + 1],
            )

        def attend(h, pool, tag):
            o_bank = pool.tile([P, T, DH], F32, name="o_bank", tag=tag)
            for t in range(T):
                nc.tensor.matmul_mx(
                    out=o_bank[:, t, :],
                    lhsT=e_codes[:, h * T + t, :].bitcast(FP8X4),
                    lhsT_scale=e_scales[:, h * T + t, :],
                    rhs=v_codes[:, h, :].bitcast(FP8X4),
                    rhs_scale=v_scales[:, h, :],
                    start=True,
                    stop=True,
                )
            cols = slice(h * DH, (h + 1) * DH)
            for t in TILE_ORDER:
                nc.vector.scalar_tensor_tensor(
                    out=y_rows(t)[:, cols],
                    in0=o_bank[:, t, :],
                    scalar=o_scale[:, h * T + t : h * T + t + 1],
                    in1=x_sb[:, t, cols],
                    op0=ALU.mult,
                    op1=ALU.add,
                )

        def tile_stats(chunk, t):
            cols = slice(STAT_EDGES[chunk] * DH, STAT_EDGES[chunk + 1] * DH)
            nc.vector.bn_stats(out=stats[:, t, chunk, :], in_=y_rows(t)[:, cols])

        def warm_up(count):
            for i in range(count):
                bank = acc_banks.tile([P, S], F32, name="warm_bank", tag="acc")
                nc.tensor.matmul(out=bank[:], lhsT=warm[:, 0:P], rhs=warm[:], start=True, stop=True)

        def attention_unit(n):
            score_matmul(n)
            find_row_max(n)
            make_exp_bias(n)
            exponentials(n)

        warm_up(WARM_MATMULS)
        for step in HEAD_ORDER.split():
            kind, arg = step[0], int(step[1:])
            if kind == "k":
                flip_k(arg)
            elif kind == "q":
                flip_q(arg)
            elif kind == "u":
                attention_unit(arg)
            elif kind == "m":
                score_matmul(arg)
            elif kind == "r":
                find_row_max(arg)
                make_exp_bias(arg)
                exponentials(arg)
            elif kind == "w":
                warm_up(arg)
            elif kind == "L":
                load_keys_and_weights(arg)
            elif kind == "g":
                regroup_keys(arg)
            elif kind == "f":
                flip_keys(arg)
            elif kind == "b":
                flip_bias()

        def live(g):
            return 0 <= g < G

        e_waiting = list(range(HEAD_UNITS))
        e_regrouped = []
        for s in range(ROUNDS):
            if live(s) and s not in keys_grouped:
                regroup_keys(s)
            n = s + HEAD_UNITS
            score_matmul(n)
            if live(s - PASS_LAG):
                for h in range(FIRST_HEADS):
                    value_pass(h, s - PASS_LAG)
            if s - PASS_LAG == G - 1:
                relu_v(0)
            if live(s + 1):
                flip_keys(s + 1)
            count = min(len(e_waiting), PER_BANK)
            flip("e", e_sb, e_waiting[0], count)
            find_row_max(n)
            for e_first, e_count in e_regrouped:
                quantise("e", e_codes, e_scales, e_first, e_count)
            e_regrouped.clear()
            make_exp_bias(n)
            exponentials(n)
            if live(s):
                quantise_keys(s)
            regroup(nc.vector.tensor_copy, "e", e_waiting[0], count)
            e_regrouped.append((e_waiting[0], count))
            e_waiting = e_waiting[count:]
            e_waiting.append(n)
            if live(s + 1) and s % PASSES_PER_LOAD == 0:
                next_load = s // PASSES_PER_LOAD + RAW_BUFS
                if next_load < LOADS:
                    load_keys_and_weights(next_load)
                elif next_load == LOADS:
                    x_sb = raw.tile([P, T, D], BF16, name="x_sb", tag="raw")
                    nc.sync.dma_start(out=x_sb[:], in_=x_rows)
                elif next_load <= LOADS + T // 2:
                    y_pair = raw.tile([P, 2, D], F32, name="y_pair", tag="raw")
                    y_pairs.append(y_pair)

        next_unit = ROUNDS + HEAD_UNITS
        waiting = [("e", next_unit - 1, 1, 0)]
        waiting += [("v", h, 1, h + 1) for h in range(FIRST_HEADS)]
        regrouped = [("e", first, count) for first, count in e_regrouped]
        quantised = set(("e", n) for n in range(e_regrouped[0][0]))
        attended = 0
        stats_due = []
        flips_done = 0

        def quantise_regrouped():
            for kind, first, count in regrouped:
                if kind == "e":
                    quantise("e", e_codes, e_scales, first, count)
                else:
                    quantise("v", v_codes, v_scales, first, count)
                for a in range(count):
                    quantised.add((kind, first + a))
            regrouped.clear()

        def run_of_flips(slot, vector_only=False):
            due = [w for w in waiting if w[3] <= slot][:FLIP_BUFS]
            for w in due:
                waiting.remove(w)
                kind, first, count, since = w
                flip(kind, e_sb if kind == "e" else v_flipped, first, count)
            for kind, first, count, since in due:
                on_vector = vector_only or kind == "v"
                regroup(nc.vector.tensor_copy if on_vector else nc.scalar.copy, kind, first, count)
                regrouped.append((kind, first, count))
                if kind == "v":
                    units = slice(first * T, (first + count) * T)
                    nc.vector.reciprocal(out=o_scale[:, units], in_=row_sums[:, units])

        for slot in range((H - FIRST_HEADS) * HEAD_SLOTS):
            head = FIRST_HEADS + slot // HEAD_SLOTS
            i = slot % HEAD_SLOTS
            n = next_unit + slot
            if n < UNITS:
                score_matmul(n)
            for g in range(i * SLOT_PASSES, (i + 1) * SLOT_PASSES):
                value_pass(head, g)
            if i == HEAD_SLOTS - 1:
                relu_v(head)
                waiting.append(("v", head, 1, slot + 1))
            if n < UNITS:
                find_row_max(n)
            ready = ("v", attended) in quantised and all(("e", attended * T + t) in quantised for t in range(T))
            quantise_regrouped()
            if n < UNITS:
                make_exp_bias(n)
                exponentials(n)
                if slot + 1 < FIRST_HEADS:
                    relu_v(slot + 1)
                if (n - next_unit) % 2 == 1 or n == UNITS - 1:
                    first = n - (n - next_unit) % 2
                    waiting.append(("e", first, n - first + 1, slot + 1))
            elif n < UNITS + T:
                t = n - UNITS
                nc.scalar.activation(
                    out=abs_unread[:], in_=x_sb[:, t, :], func=ACT.Abs, accum_out=abs_sums[:, t : t + 1]
                )
            elif n == UNITS + T:
                nc.scalar.activation(out=table_warm[:, 1:2], in_=table_warm[:, 0:1], func=ACT.Abs_reciprocal_sqrt)
                nc.vector.tensor_single_scalar(out=row_mask[:], in_=abs_sums[:], scalar=0.0, op=ALU.is_gt)
            if ready:
                attend(attended, flip_banks, "flip")
                attended += 1
                if attended in STAT_EDGES:
                    chunk = STAT_EDGES.index(attended) - 1
                    stats_due.extend((chunk, t) for t in range(T))
            if n >= UNITS:
                for due in stats_due[:STATS_PER_SLOT]:
                    tile_stats(due[0], due[1])
                del_count = min(STATS_PER_SLOT, len(stats_due))
                stats_due = stats_due[del_count:]
            if slot % FLIP_EVERY == FLIP_PHASE:
                run_of_flips(slot)
        halves = [slice(i * S, (i + 1) * S) for i in range(D // S)]

        def spread(source, i, pool, tag):
            bank = pool.tile([P, S], F32, name="row_bank", tag=tag)
            nc.tensor.matmul(out=bank[:], lhsT=ident_bf[:], rhs=source[:, halves[i]], start=True, stop=True)
            return bank

        gamma_banks = [spread(gamma_all, 0, score_banks, "score")]
        beta_banks = [spread(beta_all, i, flip_banks, "flip") for i in range(2)]
        slot = (H - FIRST_HEADS) * HEAD_SLOTS
        run_of_flips(slot, True)
        while attended < H - 1:
            attend(attended, acc_banks, "acc")
            attended += 1
            if attended in STAT_EDGES:
                chunk = STAT_EDGES.index(attended) - 1
                stats_due.extend((chunk, t) for t in range(T))
        for chunk, t in stats_due:
            tile_stats(chunk, t)
        quantise_regrouped()
        attend(H - 1, acc_banks, "acc")
        gamma_banks.append(spread(gamma_all, 1, score_banks, "score"))

        def mean_and_variance(t):
            nc.vector.bn_aggr(out=mean_var[:, t, :], in_=stats[:, t, :, :].rearrange("p c f -> p (c f)"))

        for i in range(T):
            tile_stats(len(STAT_EDGES) - 2, TILE_ORDER[i])
            if i >= 1:
                mean_and_variance(TILE_ORDER[i - 1])
            if i == 2:
                nc.vector.tensor_scalar_mul(out=minus_mean[:], in0=mean_var[:, LAST, 0:1], scalar1=-1.0)
        mean_and_variance(TILE_ORDER[T - 1])

        def centre_and_gain(t, i):
            nc.vector.scalar_tensor_tensor(
                out=y_rows(t)[:, halves[i]], in0=y_rows(t)[:, halves[i]], scalar=mean_var[:, t, 0:1],
                in1=gamma_banks[i][:], op0=ALU.subtract, op1=ALU.mult,
            )

        def normalise_and_shift(t, i):
            nc.vector.scalar_tensor_tensor(
                out=y_rows(t)[:, halves[i]], in0=y_rows(t)[:, halves[i]], scalar=out_scale[:, t : t + 1],
                in1=beta_banks[i][:], op0=ALU.mult, op1=ALU.add,
            )

        def scalar_centre(i):
            nc.scalar.activation(
                out=y_rows(LAST)[:, halves[i]], in_=y_rows(LAST)[:, halves[i]], func=ACT.Identity, bias=minus_mean[:],
                scale=1.0,
            )

        def scalar_normalise(t, i):
            nc.scalar.activation(
                out=y_rows(t)[:, halves[i]], in_=y_rows(t)[:, halves[i]], func=ACT.Copy, scale=out_scale[:, t : t + 1]
            )

        def gpsimd_row(t, i, row, op):
            nc.gpsimd.tensor_tensor(out=y_rows(t)[:, halves[i]], in0=y_rows(t)[:, halves[i]], in1=row[:, halves[i]], op=op)

        def store(t, i):
            nc.sync.dma_start(out=out_rows[:, t, halves[i]], in_=y_rows(t)[:, halves[i]])

        scalar_centre(0)
        nc.scalar.activation(
            out=rstd[:], in_=mean_var[:, :, 1:2].rearrange("p t o -> p (t o)"), func=ACT.Abs_reciprocal_sqrt,
            bias=eps[:], scale=1.0,
        )
        scalar_centre(1)
        for i in range(2):
            gpsimd_row(LAST, i, gamma_all, ALU.mult)
        centre_and_gain(0, 0)
        nc.vector.tensor_tensor(out=out_scale[:], in0=rstd[:], in1=row_mask[:], op=ALU.mult)
        pieces = [(t, i) for t in range(LAST) for i in range(2)]
        for i in range(2):
            scalar_normalise(LAST, i)
        for i in range(2):
            gpsimd_row(LAST, i, beta_all, ALU.add)
        for j in range(len(pieces)):
            if j + 1 < len(pieces):
                centre_and_gain(*pieces[j + 1])
            normalise_and_shift(*pieces[j])
            store(*pieces[j])
            if j in (2, 3):
                store(LAST, j - 2)
